import numpy as np
import ml_dtypes


def mxq(x, axis, fmt="e4m3"):
    dtype, down = {"e4m3": (ml_dtypes.float8_e4m3fn, 7), "e5m2": (ml_dtypes.float8_e5m2, 14)}[fmt]
    v = np.moveaxis(np.asarray(x, np.float32).astype(ml_dtypes.bfloat16).astype(np.float64), axis, -1)
    blocks = v.reshape(v.shape[:-1] + (-1, 32))
    amax = np.abs(blocks).max(-1, keepdims=True)
    byte = np.maximum(np.where(amax > 0, np.frexp(amax)[1] - 1 + 127, 0) - down, 1)
    scale = np.exp2(byte - 127.0)
    codes = (blocks / scale).astype(np.float32).astype(dtype).astype(np.float64)
    return np.moveaxis((codes * scale).reshape(v.shape), -1, axis)


WIDE = False


def mx_kscale(k):
    if not WIDE:
        return np.ones(k)
    levels = np.array([10, -10, 5, -5, 0])
    a = np.random.permutation(np.resize(levels, k // 512 * 4)).reshape(k // 512, 4)
    idx = np.arange(k)
    return np.exp2(a[idx // 512, idx % 128 // 32])


BF16 = ml_dtypes.bfloat16


def bf(x):
    return np.asarray(x, np.float32).astype(BF16)


def f64(x):
    return np.asarray(x).astype(np.float64)


B, T, C, H, D = 1, 512, 2048, 16, 128
HD = H * D


def unit_rms(u):
    return u / np.sqrt(np.mean(u * u, axis=-1, keepdims=True))


def setup_inputs():
    t = mx_kscale(HD)
    tv = t.reshape(H, D)
    a = (np.log(T) + 3.0) / np.sqrt(D)
    k = unit_rms(np.random.standard_normal((B, T, H, D)))
    idx = np.argsort(np.random.random((B, T, H)), axis=1)
    k_near = np.take_along_axis(k, idx[..., None], axis=1)
    q = unit_rms(a * k_near + np.sqrt(1.0 - a * a) * np.random.standard_normal((B, T, H, D)))
    return {
        "q_rot": bf(q),
        "k_rot": bf(k),
        "v": bf(np.random.standard_normal((B, T, H, D)) * 1.5 * tv),
        "v1": bf(np.random.standard_normal((B, T, H, D)) * 1.5 * tv),
        "lamb1": bf(0.5 + 0.1 * np.random.standard_normal(1)),
        "lamb2": bf(0.5 + 0.1 * np.random.standard_normal(1)),
        "wproj": bf(np.random.standard_normal((C, HD)) * 1.5 / np.sqrt(HD) / t[None, :]),
    }


def reference(q_rot, k_rot, v, v1, lamb1, lamb2, wproj):
    vm = f64(lamb1) * f64(v) + f64(lamb2) * f64(v1)
    s = f64(q_rot).transpose(0, 2, 1, 3) @ f64(k_rot).transpose(0, 2, 3, 1) * (1.0 / np.sqrt(D))
    e = np.exp(s - s.max(-1, keepdims=True))
    y = (mxq(e, 3, "e4m3") @ mxq(vm.transpose(0, 2, 1, 3), 2, "e4m3")) / e.sum(-1, keepdims=True)
    y = y.transpose(0, 2, 1, 3).reshape(B, T, HD)
    return mxq(y, 2, "e4m3") @ mxq(f64(wproj), 1, "e4m3").T

@@ -1,0 +1,450 @@
+import math
+from contextlib import ExitStack
+
+import concourse.mybir as mybir
+from concourse.masks import make_identity
+
+BF16 = mybir.dt.bfloat16
+F32 = mybir.dt.float32
+U32 = mybir.dt.uint32
+U8 = mybir.dt.uint8
+FP8X4 = mybir.dt.float8_e4m3fn_x4
+ACT = mybir.ActivationFunctionType
+ALU = mybir.AluOpType
+AXIS = mybir.AxisListType
+
+P = 128
+PACK = 4
+K_PASS = P * PACK
+TOKENS = 512
+TOKEN_TILES = TOKENS // P
+HEADS = 16
+HEAD_DIM = 128
+FEATURES = HEADS * HEAD_DIM
+GROUP = K_PASS // HEAD_DIM
+GROUPS = HEADS // GROUP
+OUT_FEATURES = 2048
+N_TILE = 512
+COL_TILES = OUT_FEATURES // N_TILE
+ROWS_PER_COL_TILE = N_TILE // P
+SCALE = 1.0 / math.sqrt(HEAD_DIM)
+
+FLOPS = 2 * 2 * HEADS * TOKENS * TOKENS * HEAD_DIM + 2 * TOKENS * FEATURES * OUT_FEATURES
+
+
+ITEMS = TOKEN_TILES * HEADS
+UNITS = ITEMS // GROUP
+W_UNITS = COL_TILES * GROUPS
+
+FIRST_SLOT = -5
+W_START = HEADS - 4
+W_READY = W_START + W_UNITS + 2
+Y_LAG = 12
+PASSES_PER_SLOT = 2
+SLOTS_PER_COL_TILE = GROUPS // PASSES_PER_SLOT
+PROJECT_SLOTS = COL_TILES * SLOTS_PER_COL_TILE
+
+
+def project_start(qt):
+    last_unit = qt * GROUPS + GROUPS - 1
+    return max(W_READY, last_unit * GROUP + Y_LAG)
+
+
+LAST_SLOT = project_start(TOKEN_TILES - 1) + PROJECT_SLOTS
+
+
+def tile_selfattention_pb_kernel(tc, q_rot, k_rot, v, v1, lamb1, lamb2, wproj, out):
+    nc = tc.nc
+
+    q_view = q_rot.rearrange("b (a p) h d -> p (b a) (h d)", p=P)
+    k_view = k_rot.rearrange("b (a p) h d -> p (b a) (h d)", p=P)
+    v_view = v.rearrange("b (a p) h d -> p (b a) (h d)", p=P)
+    v1_view = v1.rearrange("b (a p) h d -> p (b a) (h d)", p=P)
+    w_view = wproj.rearrange("(a p) k -> p a k", p=P)
+    out_view = out.rearrange("b (a p) c -> p (b a) c", p=P)
+
+    with ExitStack() as ctx:
+        keep = ctx.enter_context(tc.tile_pool(name="keep", bufs=1))
+        work = ctx.enter_context(tc.tile_pool(name="work", bufs=2))
+        psum = ctx.enter_context(tc.psum_pool(name="psum", bufs=1))
+        ctx.enter_context(tc.manual_schedule())
+
+        ident_bf = keep.tile([P, P], BF16)
+        make_identity(nc, ident_bf[:])
+        ident_f32 = keep.tile([P, P], F32)
+        make_identity(nc, ident_f32[:])
+
+        lamb1_bf = keep.tile([P, 1], BF16)
+        nc.sync.dma_start(out=lamb1_bf[:], in_=lamb1.partition_broadcast(P))
+        lamb2_bf = keep.tile([P, 1], BF16)
+        nc.sync.dma_start(out=lamb2_bf[:], in_=lamb2.partition_broadcast(P))
+        lamb1_f32 = keep.tile([P, 1], F32)
+        nc.vector.tensor_copy(out=lamb1_f32[:], in_=lamb1_bf[:])
+        lamb2_f32 = keep.tile([P, 1], F32)
+        nc.vector.tensor_copy(out=lamb2_f32[:], in_=lamb2_bf[:])
+
+        warm = keep.tile([P, 1], F32)
+        nc.scalar.activation(out=warm[:], in_=ident_f32[:, 0:1], func=ACT.Exp)
+
+        kqT = keep.tile([P, HEADS, 2 * TOKEN_TILES, P], BF16)
+        vm_codes = keep.tile([P, FEATURES], U32, align_bytes=64)
+        vm_scales = keep.tile([P, FEATURES], U8, align_bytes=64)
+        w_codes = keep.tile([P, GROUPS, OUT_FEATURES], U32, align_bytes=64)
+        w_scales = keep.tile([P, GROUPS, OUT_FEATURES], U8, align_bytes=64)
+
+        live = {}
+
+        def load_head_group(g):
+            cols = slice(g * K_PASS, (g + 1) * K_PASS)
+            k_raw = work.tile([P, TOKEN_TILES, K_PASS], BF16)
+            nc.sync.dma_start(out=k_raw[:], in_=k_view[:, :, cols])
+            q_raw = work.tile([P, TOKEN_TILES, K_PASS], BF16)
+            nc.sync.dma_start(out=q_raw[:], in_=q_view[:, :, cols])
+            v1_raw = work.tile([P, PACK, K_PASS], BF16, bufs=3)
+            nc.sync.dma_start(out=v1_raw[:], in_=v1_view[:, :, cols])
+            v_raw = work.tile([P, PACK, K_PASS], BF16, bufs=3)
+            nc.sync.dma_start(out=v_raw[:], in_=v_view[:, :, cols])
+            live[("k_raw", g)] = k_raw
+            live[("q_raw", g)] = q_raw
+            live[("v1_raw", g)] = v1_raw
+            live[("v_raw", g)] = v_raw
+
+        def load_w(ct):
+            w_raw = work.tile([P, ROWS_PER_COL_TILE, FEATURES], BF16)
+            rows = slice(ct * ROWS_PER_COL_TILE, (ct + 1) * ROWS_PER_COL_TILE)
+            nc.sync.dma_start(out=w_raw[:], in_=w_view[:, rows, :])
+            live[("w_raw", ct)] = w_raw
+
+        def transpose_kq(h):
+            if not 0 <= h < HEADS:
+                return
+            g, j = divmod(h, GROUP)
+            d_cols = slice(j * HEAD_DIM, (j + 1) * HEAD_DIM)
+            kq_ps = psum.tile([P, 2 * TOKEN_TILES, P], BF16, tag="x", bufs=2)
+            for a in range(TOKEN_TILES):
+                nc.tensor.transpose(kq_ps[:, a, :], live[("k_raw", g)][:, a, d_cols], ident_bf[:])
+            for a in range(TOKEN_TILES):
+                nc.tensor.transpose(
+                    kq_ps[:, TOKEN_TILES + a, :], live[("q_raw", g)][:, a, d_cols], ident_bf[:]
+                )
+            live[("kq_ps", h)] = kq_ps
+
+        def keep_kq(h):
+            if not 0 <= h < HEADS:
+                return
+            nc.scalar.copy(out=kqT[:, h, :, :], in_=live[("kq_ps", h)][:])
+
+        def scale_v1(h):
+            if not 0 <= h < HEADS:
+                return
+            g, j = divmod(h, GROUP)
+            d_cols = slice(j * HEAD_DIM, (j + 1) * HEAD_DIM)
+            scaled_v1 = work.tile([P, PACK, HEAD_DIM], F32)
+            nc.gpsimd.tensor_scalar(
+                out=scaled_v1[:], in0=live[("v1_raw", g)][:, :, d_cols],
+                scalar1=lamb2_f32[:, 0:1], scalar2=0.0, op0=ALU.mult, op1=ALU.add,
+            )
+            live[("scaled_v1", h)] = scaled_v1
+
+        def mix_values(h):
+            if not 0 <= h < HEADS:
+                return
+            g, j = divmod(h, GROUP)
+            d_cols = slice(j * HEAD_DIM, (j + 1) * HEAD_DIM)
+            vm_grouped = work.tile([P, HEAD_DIM, PACK], BF16, align_bytes=64)
+            nc.vector.scalar_tensor_tensor(
+                out=vm_grouped[:],
+                in0=live[("v_raw", g)][:, :, d_cols].rearrange("p t c -> p c t"),
+                scalar=lamb1_f32[:, 0:1],
+                in1=live[("scaled_v1", h)][:].rearrange("p t c -> p c t"),
+                op0=ALU.mult, op1=ALU.add,
+            )
+            live[("vm_grouped", h)] = vm_grouped
+
+        def quantise_values(h):
+            if not 0 <= h < HEADS:
+                return
+            cols = slice(h * HEAD_DIM, (h + 1) * HEAD_DIM)
+            nc.vector.quantize_mx(
+                out=vm_codes[:, cols].bitcast(FP8X4),
+                scales=vm_scales[:, cols],
+                in_=live[("vm_grouped", h)][:].rearrange("p c t -> p (c t)"),
+            )
+
+        def transpose_w(wu):
+            if not 0 <= wu < W_UNITS:
+                return
+            ct, g = divmod(wu, GROUPS)
+            w_words = live[("w_raw", ct)][:].rearrange("p a k -> p (a k)").bitcast(F32)
+            words_per_row = FEATURES // 2
+            for half in range(2):
+                wt_ps = psum.tile([P, 2, 2, P], F32, tag="x", bufs=2)
+                for i in range(2):
+                    for u in range(2):
+                        first = (2 * half + i) * words_per_row + (2 * g + u) * P
+                        nc.tensor.transpose(
+                            wt_ps[:, i, u, :], w_words[:, first : first + P], ident_f32[:]
+                        )
+                live[("wt_ps", wu, half)] = wt_ps
+
+        def regroup_w(wu):
+            if not 0 <= wu < W_UNITS:
+                return
+            w_grouped = work.tile([P, N_TILE, PACK], BF16, align_bytes=64, bufs=3)
+            grouped_words = (
+                w_grouped[:].rearrange("p c t -> p (c t)").bitcast(F32)
+                .rearrange("p (a c u) -> p a c u", a=ROWS_PER_COL_TILE, u=2)
+            )
+            nc.scalar.copy(
+                out=grouped_words[:, 0:2, :, :],
+                in_=live[("wt_ps", wu, 0)][:].rearrange("p a u c -> p a c u"),
+            )
+            if wu % 2 == 0:
+                nc.scalar.copy(
+                    out=grouped_words[:, 2:4, :, :],
+                    in_=live[("wt_ps", wu, 1)][:].rearrange("p a u c -> p a c u"),
+                )
+            else:
+                nc.vector.tensor_copy(
+                    out=grouped_words[:, 2:4, :, :],
+                    in_=live[("wt_ps", wu, 1)][:].rearrange("p a u c -> p a c u"),
+                )
+            live[("w_grouped", wu)] = w_grouped
+
+        def quantise_w(wu):
+            if not 0 <= wu < W_UNITS:
+                return
+            ct, g = divmod(wu, GROUPS)
+            cols = slice(ct * N_TILE, (ct + 1) * N_TILE)
+            nc.vector.quantize_mx(
+                out=w_codes[:, g, cols].bitcast(FP8X4),
+                scales=w_scales[:, g, cols],
+                in_=live[("w_grouped", wu)][:].rearrange("p c t -> p (c t)"),
+            )
+
+        def scores(i):
+            if not 0 <= i < ITEMS:
+                return
+            qt, h = divmod(i, HEADS)
+            s_ps = psum.tile([P, TOKENS], F32, tag="s", bufs=4)
+            nc.tensor.matmul(
+                out=s_ps[:],
+                lhsT=kqT[:, h, TOKEN_TILES + qt, :],
+                rhs=kqT[:, h, 0:TOKEN_TILES, :].rearrange("p a t -> p (a t)"),
+                start=True, stop=True,
+            )
+            live[("s_ps", i)] = s_ps
+
+        def row_maximum(i):
+            if not 0 <= i < ITEMS:
+                return
+            n, j = divmod(i, GROUP)
+            if j == 0:
+                row_max = work.tile([P, GROUP], F32)
+                live[("row_max", n)] = row_max
+            nc.vector.reduce_max(
+                out=live[("row_max", n)][:, j : j + 1], in_=live[("s_ps", i)][:], axis=AXIS.X
+            )
+
+        def exp_bias_of(i):
+            if not 0 <= i < ITEMS:
+                return
+            n, j = divmod(i, GROUP)
+            if j == 0:
+                exp_bias = work.tile([P, GROUP], F32)
+                live[("exp_bias", n)] = exp_bias
+            nc.vector.tensor_scalar_mul(
+                out=live[("exp_bias", n)][:, j : j + 1],
+                in0=live[("row_max", n)][:, j : j + 1],
+                scalar1=-SCALE,
+            )
+
+        def exponentials(i):
+            if not 0 <= i < ITEMS:
+                return
+            n, j = divmod(i, GROUP)
+            if j == 0:
+                row_sum = work.tile([P, GROUP], F32, bufs=3)
+                live[("row_sum", n)] = row_sum
+            e_sb = work.tile([P, TOKENS], BF16, bufs=3)
+            nc.scalar.activation(
+                out=e_sb[:], in_=live[("s_ps", i)][:], func=ACT.Exp,
+                bias=live[("exp_bias", n)][:, j : j + 1], scale=SCALE,
+                accum_out=live[("row_sum", n)][:, j : j + 1],
+            )
+            live[("e_sb", i)] = e_sb
+
+        def transpose_e(i):
+            if not 0 <= i < ITEMS:
+                return
+            et_ps = psum.tile([P, PACK, P], BF16, tag="et", bufs=1)
+            for t in range(PACK):
+                nc.tensor.transpose(
+                    et_ps[:, t, :], live[("e_sb", i)][:, t * P : (t + 1) * P], ident_bf[:]
+                )
+            live[("et_ps", i)] = et_ps
+
+        def regroup_e(i):
+            if not 0 <= i < ITEMS:
+                return
+            n, j = divmod(i, GROUP)
+            if j == 0:
+                e_grouped = work.tile([P, GROUP, P, PACK], BF16, align_bytes=64)
+                live[("e_grouped", n)] = e_grouped
+            nc.scalar.copy(
+                out=live[("e_grouped", n)][:, j, :, :],
+                in_=live[("et_ps", i)][:].rearrange("p t q -> p q t"),
+            )
+
+        def unit_at(slot):
+            if slot % GROUP == 0 and 0 <= slot < ITEMS:
+                return slot // GROUP
+            return -1
+
+        def quantise_e(n):
+            if n < 0:
+                return
+            e_codes = work.tile([P, GROUP * P], U32, align_bytes=64)
+            e_scales = work.tile([P, GROUP * P], U8, align_bytes=64)
+            nc.vector.quantize_mx(
+                out=e_codes[:].bitcast(FP8X4),
+                scales=e_scales[:],
+                in_=live[("e_grouped", n)][:].rearrange("p h q t -> p (h q t)"),
+            )
+            live[("e_codes", n)] = e_codes
+            live[("e_scales", n)] = e_scales
+
+        def multiply_values(n):
+            if n < 0:
+                return
+            g = n % GROUPS
+            y_ps = psum.tile([P, GROUP, HEAD_DIM], F32, tag="y", bufs=1)
+            for j in range(GROUP):
+                h = g * GROUP + j
+                q_cols = slice(j * P, (j + 1) * P)
+                d_cols = slice(h * HEAD_DIM, (h + 1) * HEAD_DIM)
+                nc.tensor.matmul_mx(
+                    out=y_ps[:, j, :],
+                    lhsT=live[("e_codes", n)][:, q_cols].bitcast(FP8X4),
+                    lhsT_scale=live[("e_scales", n)][:, q_cols],
+                    rhs=vm_codes[:, d_cols].bitcast(FP8X4),
+                    rhs_scale=vm_scales[:, d_cols],
+                    start=True, stop=True,
+                )
+            live[("y_ps", n)] = y_ps
+
+        def normalise(n):
+            if n < 0:
+                return
+            qt, g = divmod(n, GROUPS)
+            if g == 0:
+                y_bf = work.tile([P, FEATURES], BF16)
+                live[("y_bf", qt)] = y_bf
+            inv_sum = work.tile([P, GROUP], F32)
+            nc.vector.reciprocal(out=inv_sum[:], in_=live[("row_sum", n)][:])
+            nc.vector.tensor_tensor(
+                out=live[("y_bf", qt)][:, g * K_PASS : (g + 1) * K_PASS]
+                .rearrange("q (h d) -> q h d", h=GROUP),
+                in0=live[("y_ps", n)][:],
+                in1=inv_sum[:].unsqueeze(2).to_broadcast([P, GROUP, HEAD_DIM]),
+                op=ALU.mult,
+            )
+
+        def transpose_y(n):
+            if n < 0:
+                return
+            qt, g = divmod(n, GROUPS)
+            y_planes = live[("y_bf", qt)][:].rearrange(
+                "q (g u p e) -> q g u e p", g=GROUPS, u=2, e=2
+            )
+            yt_ps = psum.tile([P, PACK, P], BF16, tag="y", bufs=1)
+            for u in range(2):
+                for e in range(2):
+                    nc.tensor.transpose(yt_ps[:, 2 * u + e, :], y_planes[:, g, u, e, :], ident_bf[:])
+            live[("yt_ps", n)] = yt_ps
+
+        def regroup_y(n):
+            if n < 0:
+                return
+            y_grouped = work.tile([P, P, PACK], BF16, align_bytes=64)
+            nc.vector.tensor_copy(
+                out=y_grouped[:], in_=live[("yt_ps", n)][:].rearrange("p t q -> p q t")
+            )
+            live[("y_grouped", n)] = y_grouped
+
+        def quantise_y(n):
+            if n < 0:
+                return
+            qt, g = divmod(n, GROUPS)
+            if g == 0:
+                y_codes = work.tile([P, GROUPS * P], U32, align_bytes=64)
+                y_scales = work.tile([P, GROUPS * P], U8, align_bytes=64)
+                live[("y_codes", qt)] = y_codes
+                live[("y_scales", qt)] = y_scales
+            t_cols = slice(g * P, (g + 1) * P)
+            nc.vector.quantize_mx(
+                out=live[("y_codes", qt)][:, t_cols].bitcast(FP8X4),
+                scales=live[("y_scales", qt)][:, t_cols],
+                in_=live[("y_grouped", n)][:].rearrange("p q t -> p (q t)"),
+            )
+
+        def project(qt, step):
+            if not 0 <= step < PROJECT_SLOTS:
+                return
+            ct, part = divmod(step, SLOTS_PER_COL_TILE)
+            cols = slice(ct * N_TILE, (ct + 1) * N_TILE)
+            if part == 0:
+                o_ps = psum.tile([P, N_TILE], F32, tag="x", bufs=2)
+                live[("o_ps", qt, ct)] = o_ps
+            for g in range(part * PASSES_PER_SLOT, (part + 1) * PASSES_PER_SLOT):
+                t_cols = slice(g * P, (g + 1) * P)
+                nc.tensor.matmul_mx(
+                    out=live[("o_ps", qt, ct)][:],
+                    lhsT=live[("y_codes", qt)][:, t_cols].bitcast(FP8X4),
+                    lhsT_scale=live[("y_scales", qt)][:, t_cols],
+                    rhs=w_codes[:, g, cols].bitcast(FP8X4),
+                    rhs_scale=w_scales[:, g, cols],
+                    start=(g == 0), stop=(g == GROUPS - 1),
+                )
+
+        def store_out(qt, step):
+            if step % SLOTS_PER_COL_TILE != 0 or not 0 < step <= PROJECT_SLOTS:
+                return
+            ct = step // SLOTS_PER_COL_TILE - 1
+            o_sb = work.tile([P, N_TILE], F32, bufs=3)
+            if ct % 2 == 0:
+                nc.vector.tensor_copy(out=o_sb[:], in_=live[("o_ps", qt, ct)][:])
+            else:
+                nc.scalar.copy(out=o_sb[:], in_=live[("o_ps", qt, ct)][:])
+            nc.sync.dma_start(out=out_view[:, qt, ct * N_TILE : (ct + 1) * N_TILE], in_=o_sb[:])
+
+        for g in range(GROUPS):
+            load_head_group(g)
+        for ct in range(COL_TILES):
+            load_w(ct)
+
+        for s in range(FIRST_SLOT, LAST_SLOT + 1):
+            regroup_e(s - 2)
+            keep_kq(s + 4)
+            regroup_w(s - W_START - 1)
+            for qt in range(TOKEN_TILES):
+                store_out(qt, s - project_start(qt))
+            exponentials(s)
+            exp_bias_of(s + 1)
+            row_maximum(s + 2)
+            quantise_e(unit_at(s - 6))
+            normalise(unit_at(s - 8))
+            regroup_y(unit_at(s - 10))
+            quantise_y(unit_at(s - 11))
+            mix_values(s)
+            quantise_values(s - 1)
+            quantise_w(s - W_START - 2)
+            scale_v1(s + 1)
+            scores(s + 3)
+            transpose_e(s - 1)
+            transpose_y(unit_at(s - 9))
+            transpose_kq(s + 5)
+            transpose_w(s - W_START)
+            multiply_values(unit_at(s - 7))
+            for qt in range(TOKEN_TILES):
+                project(qt, s - project_start(qt))

@@ -43,6 +43,7 @@ Y_LAG = 12
 PASSES_PER_SLOT = 2
 SLOTS_PER_COL_TILE = GROUPS // PASSES_PER_SLOT
 PROJECT_SLOTS = COL_TILES * SLOTS_PER_COL_TILE
+LAST_TILE = TOKEN_TILES - 1
 
 
 def project_start(qt):
@@ -50,7 +51,11 @@ def project_start(qt):
     return max(W_READY, last_unit * GROUP + Y_LAG)
 
 
-LAST_SLOT = project_start(TOKEN_TILES - 1) + PROJECT_SLOTS
+def last_tile_slot(g):
+    return max(ITEMS, (LAST_TILE * GROUPS + g) * GROUP + Y_LAG)
+
+
+LAST_SLOT = last_tile_slot(GROUPS - 1)
 
 
 def tile_selfattention_pb_kernel(tc, q_rot, k_rot, v, v1, lamb1, lamb2, wproj, out):
@@ -94,18 +99,21 @@ def tile_selfattention_pb_kernel(tc, q_rot, k_rot, v, v1, lamb1, lamb2, wproj, o
 
         live = {}
 
-        def load_head_group(g):
+        def load_kq(g):
             cols = slice(g * K_PASS, (g + 1) * K_PASS)
             k_raw = work.tile([P, TOKEN_TILES, K_PASS], BF16)
             nc.sync.dma_start(out=k_raw[:], in_=k_view[:, :, cols])
             q_raw = work.tile([P, TOKEN_TILES, K_PASS], BF16)
             nc.sync.dma_start(out=q_raw[:], in_=q_view[:, :, cols])
+            live[("k_raw", g)] = k_raw
+            live[("q_raw", g)] = q_raw
+
+        def load_values(g):
+            cols = slice(g * K_PASS, (g + 1) * K_PASS)
             v1_raw = work.tile([P, PACK, K_PASS], BF16, bufs=3)
             nc.sync.dma_start(out=v1_raw[:], in_=v1_view[:, :, cols])
             v_raw = work.tile([P, PACK, K_PASS], BF16, bufs=3)
             nc.sync.dma_start(out=v_raw[:], in_=v_view[:, :, cols])
-            live[("k_raw", g)] = k_raw
-            live[("q_raw", g)] = q_raw
             live[("v1_raw", g)] = v1_raw
             live[("v_raw", g)] = v_raw
 
@@ -253,10 +261,10 @@ def tile_selfattention_pb_kernel(tc, q_rot, k_rot, v, v1, lamb1, lamb2, wproj, o
             if j == 0:
                 exp_bias = work.tile([P, GROUP], F32)
                 live[("exp_bias", n)] = exp_bias
-            nc.vector.tensor_scalar_mul(
+            nc.gpsimd.tensor_scalar(
                 out=live[("exp_bias", n)][:, j : j + 1],
                 in0=live[("row_max", n)][:, j : j + 1],
-                scalar1=-SCALE,
+                scalar1=-SCALE, scalar2=0.0, op0=ALU.mult, op1=ALU.add,
             )
 
         def exponentials(i):
@@ -407,19 +415,41 @@ def tile_selfattention_pb_kernel(tc, q_rot, k_rot, v, v1, lamb1, lamb2, wproj, o
                     start=(g == 0), stop=(g == GROUPS - 1),
                 )
 
-        def store_out(qt, step):
-            if step % SLOTS_PER_COL_TILE != 0 or not 0 < step <= PROJECT_SLOTS:
-                return
-            ct = step // SLOTS_PER_COL_TILE - 1
-            o_sb = work.tile([P, N_TILE], F32, bufs=3)
+        def store_after(qt, step):
+            if step % SLOTS_PER_COL_TILE == 0 and 0 < step <= PROJECT_SLOTS:
+                store_out(qt, step // SLOTS_PER_COL_TILE - 1)
+
+        def store_out(qt, ct):
+            o_sb = work.tile([P, N_TILE], F32, bufs=COL_TILES)
             if ct % 2 == 0:
                 nc.vector.tensor_copy(out=o_sb[:], in_=live[("o_ps", qt, ct)][:])
             else:
                 nc.scalar.copy(out=o_sb[:], in_=live[("o_ps", qt, ct)][:])
             nc.sync.dma_start(out=out_view[:, qt, ct * N_TILE : (ct + 1) * N_TILE], in_=o_sb[:])
 
+        def project_last_tile(g):
+            if not 0 <= g < GROUPS:
+                return
+            t_cols = slice(g * P, (g + 1) * P)
+            for ct in range(COL_TILES):
+                if g == 0:
+                    o_ps = psum.tile([P, N_TILE], F32, tag="s", bufs=4)
+                    live[("o_ps", LAST_TILE, ct)] = o_ps
+                cols = slice(ct * N_TILE, (ct + 1) * N_TILE)
+                nc.tensor.matmul_mx(
+                    out=live[("o_ps", LAST_TILE, ct)][:],
+                    lhsT=live[("y_codes", LAST_TILE)][:, t_cols].bitcast(FP8X4),
+                    lhsT_scale=live[("y_scales", LAST_TILE)][:, t_cols],
+                    rhs=w_codes[:, g, cols].bitcast(FP8X4),
+                    rhs_scale=w_scales[:, g, cols],
+                    start=(g == 0), stop=(g == GROUPS - 1),
+                )
+
+        load_kq(0)
         for g in range(GROUPS):
-            load_head_group(g)
+            if g + 1 < GROUPS:
+                load_kq(g + 1)
+            load_values(g)
         for ct in range(COL_TILES):
             load_w(ct)
 
@@ -427,24 +457,29 @@ def tile_selfattention_pb_kernel(tc, q_rot, k_rot, v, v1, lamb1, lamb2, wproj, o
             regroup_e(s - 2)
             keep_kq(s + 4)
             regroup_w(s - W_START - 1)
-            for qt in range(TOKEN_TILES):
-                store_out(qt, s - project_start(qt))
+            for qt in range(LAST_TILE):
+                store_after(qt, s - project_start(qt))
             exponentials(s)
-            exp_bias_of(s + 1)
             row_maximum(s + 2)
             quantise_e(unit_at(s - 6))
             normalise(unit_at(s - 8))
             regroup_y(unit_at(s - 10))
             quantise_y(unit_at(s - 11))
-            mix_values(s)
-            quantise_values(s - 1)
+            mix_values(s - 2)
+            quantise_values(s - 3)
             quantise_w(s - W_START - 2)
-            scale_v1(s + 1)
+            exp_bias_of(s + 1)
+            scale_v1(s - 1)
             scores(s + 3)
             transpose_e(s - 1)
             transpose_y(unit_at(s - 9))
             transpose_kq(s + 5)
             transpose_w(s - W_START)
             multiply_values(unit_at(s - 7))
-            for qt in range(TOKEN_TILES):
+            for qt in range(LAST_TILE):
                 project(qt, s - project_start(qt))
+            for g in range(GROUPS):
+                if s == last_tile_slot(g):
+                    project_last_tile(g)
+        for ct in range(COL_TILES):
+            store_out(LAST_TILE, ct)

@@ -43,6 +43,7 @@ Y_LAG = 12
 PASSES_PER_SLOT = 2
 SLOTS_PER_COL_TILE = GROUPS // PASSES_PER_SLOT
 PROJECT_SLOTS = COL_TILES * SLOTS_PER_COL_TILE
+STORE_LAG = 2
 LAST_TILE = TOKEN_TILES - 1
 
 
@@ -416,15 +417,13 @@ def tile_selfattention_pb_kernel(tc, q_rot, k_rot, v, v1, lamb1, lamb2, wproj, o
                 )
 
         def store_after(qt, step):
-            if step % SLOTS_PER_COL_TILE == 0 and 0 < step <= PROJECT_SLOTS:
-                store_out(qt, step // SLOTS_PER_COL_TILE - 1)
+            done = step - STORE_LAG + 1
+            if done % SLOTS_PER_COL_TILE == 0 and 0 < done <= PROJECT_SLOTS:
+                store_out(qt, done // SLOTS_PER_COL_TILE - 1, nc.vector.tensor_copy)
 
-        def store_out(qt, ct):
+        def store_out(qt, ct, copy):
             o_sb = work.tile([P, N_TILE], F32, bufs=COL_TILES)
-            if ct % 2 == 0:
-                nc.vector.tensor_copy(out=o_sb[:], in_=live[("o_ps", qt, ct)][:])
-            else:
-                nc.scalar.copy(out=o_sb[:], in_=live[("o_ps", qt, ct)][:])
+            copy(out=o_sb[:], in_=live[("o_ps", qt, ct)][:])
             nc.sync.dma_start(out=out_view[:, qt, ct * N_TILE : (ct + 1) * N_TILE], in_=o_sb[:])
 
         def project_last_tile(g):
@@ -455,11 +454,11 @@ def tile_selfattention_pb_kernel(tc, q_rot, k_rot, v, v1, lamb1, lamb2, wproj, o
 
         for s in range(FIRST_SLOT, LAST_SLOT + 1):
             regroup_e(s - 2)
-            keep_kq(s + 4)
             regroup_w(s - W_START - 1)
             for qt in range(LAST_TILE):
                 store_after(qt, s - project_start(qt))
             exponentials(s)
+            keep_kq(s + 4)
             row_maximum(s + 2)
             quantise_e(unit_at(s - 6))
             normalise(unit_at(s - 8))
@@ -482,4 +481,4 @@ def tile_selfattention_pb_kernel(tc, q_rot, k_rot, v, v1, lamb1, lamb2, wproj, o
                 if s == last_tile_slot(g):
                     project_last_tile(g)
         for ct in range(COL_TILES):
-            store_out(LAST_TILE, ct)
+            store_out(LAST_TILE, ct, nc.vector.tensor_copy if ct % 2 == 0 else nc.scalar.copy)

@@ -286,7 +286,7 @@ def tile_selfattention_pb_kernel(tc, q_rot, k_rot, v, v1, lamb1, lamb2, wproj, o
         def transpose_e(i):
             if not 0 <= i < ITEMS:
                 return
-            et_ps = psum.tile([P, PACK, P], BF16, tag="et", bufs=1)
+            et_ps = psum.tile([P, PACK, P], BF16, tag="small", bufs=2)
             for t in range(PACK):
                 nc.tensor.transpose(
                     et_ps[:, t, :], live[("e_sb", i)][:, t * P : (t + 1) * P], ident_bf[:]
@@ -327,7 +327,7 @@ def tile_selfattention_pb_kernel(tc, q_rot, k_rot, v, v1, lamb1, lamb2, wproj, o
             if n < 0:
                 return
             g = n % GROUPS
-            y_ps = psum.tile([P, GROUP, HEAD_DIM], F32, tag="y", bufs=1)
+            y_ps = psum.tile([P, GROUP, HEAD_DIM], F32, tag="small", bufs=2)
             for j in range(GROUP):
                 h = g * GROUP + j
                 q_cols = slice(j * P, (j + 1) * P)
@@ -366,7 +366,7 @@ def tile_selfattention_pb_kernel(tc, q_rot, k_rot, v, v1, lamb1, lamb2, wproj, o
             y_planes = live[("y_bf", qt)][:].rearrange(
                 "q (g u p e) -> q g u e p", g=GROUPS, u=2, e=2
             )
-            yt_ps = psum.tile([P, PACK, P], BF16, tag="y", bufs=1)
+            yt_ps = psum.tile([P, PACK, P], BF16, tag="small", bufs=2)
             for u in range(2):
                 for e in range(2):
                     nc.tensor.transpose(yt_ps[:, 2 * u + e, :], y_planes[:, g, u, e, :], ident_bf[:])

@@ -64,8 +64,8 @@ def tile_selfattention_pb_kernel(tc, q_rot, k_rot, v, v1, lamb1, lamb2, wproj, o
 
     q_view = q_rot.rearrange("b (a p) h d -> p (b a) (h d)", p=P)
     k_view = k_rot.rearrange("b (a p) h d -> p (b a) (h d)", p=P)
-    v_view = v.rearrange("b (a p) h d -> p (b a) (h d)", p=P)
-    v1_view = v1.rearrange("b (a p) h d -> p (b a) (h d)", p=P)
+    v_view = v.rearrange("b (u p e) h d -> p (b u) e (h d)", u=2, e=2)
+    v1_view = v1.rearrange("b (u p e) h d -> p (b u) e (h d)", u=2, e=2)
     w_view = wproj.rearrange("(a p) k -> p a k", p=P)
     out_view = out.rearrange("b (a p) c -> p (b a) c", p=P)
 
@@ -112,9 +112,11 @@ def tile_selfattention_pb_kernel(tc, q_rot, k_rot, v, v1, lamb1, lamb2, wproj, o
         def load_values(g):
             cols = slice(g * K_PASS, (g + 1) * K_PASS)
             v1_raw = work.tile([P, PACK, K_PASS], BF16, bufs=3)
-            nc.sync.dma_start(out=v1_raw[:], in_=v1_view[:, :, cols])
+            for u in range(2):
+                nc.sync.dma_start(out=v1_raw[:, 2 * u : 2 * u + 2, :], in_=v1_view[:, u, :, cols])
             v_raw = work.tile([P, PACK, K_PASS], BF16, bufs=3)
-            nc.sync.dma_start(out=v_raw[:], in_=v_view[:, :, cols])
+            for u in range(2):
+                nc.sync.dma_start(out=v_raw[:, 2 * u : 2 * u + 2, :], in_=v_view[:, u, :, cols])
             live[("v1_raw", g)] = v1_raw
             live[("v_raw", g)] = v_raw
 
@@ -286,11 +288,10 @@ def tile_selfattention_pb_kernel(tc, q_rot, k_rot, v, v1, lamb1, lamb2, wproj, o
         def transpose_e(i):
             if not 0 <= i < ITEMS:
                 return
-            et_ps = psum.tile([P, PACK, P], BF16, tag="small", bufs=2)
-            for t in range(PACK):
-                nc.tensor.transpose(
-                    et_ps[:, t, :], live[("e_sb", i)][:, t * P : (t + 1) * P], ident_bf[:]
-                )
+            et_ps = psum.tile([P, 2, P], F32, tag="small", bufs=2)
+            e_words = live[("e_sb", i)][:].bitcast(F32)
+            for u in range(2):
+                nc.tensor.transpose(et_ps[:, u, :], e_words[:, u * P : (u + 1) * P], ident_f32[:])
             live[("et_ps", i)] = et_ps
 
         def regroup_e(i):
@@ -300,9 +301,12 @@ def tile_selfattention_pb_kernel(tc, q_rot, k_rot, v, v1, lamb1, lamb2, wproj, o
             if j == 0:
                 e_grouped = work.tile([P, GROUP, P, PACK], BF16, align_bytes=64)
                 live[("e_grouped", n)] = e_grouped
+            grouped_words = (
+                live[("e_grouped", n)][:].rearrange("p h q t -> p (h q t)").bitcast(F32)
+                .rearrange("p (h q u) -> p h q u", h=GROUP, u=2)
+            )
             nc.scalar.copy(
-                out=live[("e_grouped", n)][:, j, :, :],
-                in_=live[("et_ps", i)][:].rearrange("p t q -> p q t"),
+                out=grouped_words[:, j, :, :], in_=live[("et_ps", i)][:].rearrange("p u q -> p q u")
             )
 
         def unit_at(slot):

@@ -89,6 +89,11 @@ def tile_selfattention_pb_kernel(tc, q_rot, k_rot, v, v1, lamb1, lamb2, wproj, o
         lamb2_f32 = keep.tile([P, 1], F32)
         nc.vector.tensor_copy(out=lamb2_f32[:], in_=lamb2_bf[:])
 
+        lamb2_diag = keep.tile([P, P], BF16)
+        nc.vector.tensor_scalar(
+            out=lamb2_diag[:], in0=ident_bf[:], scalar1=lamb2_f32[:, 0:1], scalar2=None, op0=ALU.mult
+        )
+
         warm = keep.tile([P, 1], F32)
         nc.scalar.activation(out=warm[:], in_=ident_f32[:, 0:1], func=ACT.Exp)
 
@@ -150,12 +155,12 @@ def tile_selfattention_pb_kernel(tc, q_rot, k_rot, v, v1, lamb1, lamb2, wproj, o
                 return
             g, j = divmod(h, GROUP)
             d_cols = slice(j * HEAD_DIM, (j + 1) * HEAD_DIM)
-            scaled_v1 = work.tile([P, PACK, HEAD_DIM], F32)
-            nc.gpsimd.tensor_scalar(
-                out=scaled_v1[:], in0=live[("v1_raw", g)][:, :, d_cols],
-                scalar1=lamb2_f32[:, 0:1], scalar2=0.0, op0=ALU.mult, op1=ALU.add,
+            v1_ps = psum.tile([P, PACK, HEAD_DIM], F32, tag="x", bufs=2)
+            nc.tensor.matmul(
+                out=v1_ps[:], lhsT=lamb2_diag[:], rhs=live[("v1_raw", g)][:, :, d_cols],
+                start=True, stop=True,
             )
-            live[("scaled_v1", h)] = scaled_v1
+            live[("scaled_v1", h)] = v1_ps
 
         def mix_values(h):
             if not 0 <= h < HEADS:
@@ -355,25 +360,22 @@ def tile_selfattention_pb_kernel(tc, q_rot, k_rot, v, v1, lamb1, lamb2, wproj, o
                 live[("y_bf", qt)] = y_bf
             inv_sum = work.tile([P, GROUP], F32)
             nc.vector.reciprocal(out=inv_sum[:], in_=live[("row_sum", n)][:])
-            nc.vector.tensor_tensor(
-                out=live[("y_bf", qt)][:, g * K_PASS : (g + 1) * K_PASS]
-                .rearrange("q (h d) -> q h d", h=GROUP),
-                in0=live[("y_ps", n)][:],
-                in1=inv_sum[:].unsqueeze(2).to_broadcast([P, GROUP, HEAD_DIM]),
-                op=ALU.mult,
-            )
+            for j in range(GROUP):
+                first = g * K_PASS + j * HEAD_DIM
+                nc.scalar.activation(
+                    out=live[("y_bf", qt)][:, first : first + HEAD_DIM],
+                    in_=live[("y_ps", n)][:, j, :], func=ACT.Copy, scale=inv_sum[:, j : j + 1],
+                )
 
         def transpose_y(n):
             if n < 0:
                 return
             qt, g = divmod(n, GROUPS)
-            y_planes = live[("y_bf", qt)][:].rearrange(
-                "q (g u p e) -> q g u e p", g=GROUPS, u=2, e=2
-            )
-            yt_ps = psum.tile([P, PACK, P], BF16, tag="small", bufs=2)
+            y_words = live[("y_bf", qt)][:].bitcast(F32)
+            yt_ps = psum.tile([P, 2, P], F32, tag="small", bufs=2)
             for u in range(2):
-                for e in range(2):
-                    nc.tensor.transpose(yt_ps[:, 2 * u + e, :], y_planes[:, g, u, e, :], ident_bf[:])
+                first = (2 * g + u) * P
+                nc.tensor.transpose(yt_ps[:, u, :], y_words[:, first : first + P], ident_f32[:])
             live[("yt_ps", n)] = yt_ps
 
         def regroup_y(n):
@@ -381,7 +383,9 @@ def tile_selfattention_pb_kernel(tc, q_rot, k_rot, v, v1, lamb1, lamb2, wproj, o
                 return
             y_grouped = work.tile([P, P, PACK], BF16, align_bytes=64)
             nc.vector.tensor_copy(
-                out=y_grouped[:], in_=live[("yt_ps", n)][:].rearrange("p t q -> p q t")
+                out=y_grouped[:].rearrange("p q t -> p (q t)").bitcast(F32)
+                .rearrange("p (q u) -> p q u", u=2),
+                in_=live[("yt_ps", n)][:].rearrange("p u q -> p q u"),
             )
             live[("y_grouped", n)] = y_grouped
 
@@ -472,11 +476,11 @@ def tile_selfattention_pb_kernel(tc, q_rot, k_rot, v, v1, lamb1, lamb2, wproj, o
             quantise_values(s - 3)
             quantise_w(s - W_START - 2)
             exp_bias_of(s + 1)
-            scale_v1(s - 1)
             scores(s + 3)
             transpose_e(s - 1)
             transpose_y(unit_at(s - 9))
             transpose_kq(s + 5)
+            scale_v1(s - 1)
             transpose_w(s - W_START)
             multiply_values(unit_at(s - 7))
             for qt in range(LAST_TILE):

@@ -36,24 +36,39 @@ ITEMS = TOKEN_TILES * HEADS
 UNITS = ITEMS // GROUP
 W_UNITS = COL_TILES * GROUPS
 
-FIRST_SLOT = -5
-W_START = HEADS - 4
-W_READY = W_START + W_UNITS + 2
-Y_LAG = 12
-PASSES_PER_SLOT = 2
-SLOTS_PER_COL_TILE = GROUPS // PASSES_PER_SLOT
-PROJECT_SLOTS = COL_TILES * SLOTS_PER_COL_TILE
-STORE_LAG = 2
+FIRST_SLOT = -4
+W_START = HEADS - 3
+Y_LAG = 11
 LAST_TILE = TOKEN_TILES - 1
 
 
-def project_start(qt):
-    last_unit = qt * GROUPS + GROUPS - 1
-    return max(W_READY, last_unit * GROUP + Y_LAG)
+def y_ready(n):
+    return n * GROUP + Y_LAG
+
+
+def w_ready(ct):
+    return W_START + 2 * (ct + 1) * GROUPS + 2
+
+
+def projection_slots():
+    jobs = []
+    for qt in range(LAST_TILE):
+        for ct in range(COL_TILES):
+            jobs.append((max(y_ready(qt * GROUPS + GROUPS - 1), w_ready(ct)), qt, ct))
+    slots = {}
+    free = 0
+    for ready, qt, ct in sorted(jobs):
+        slot = max(free, ready + ready % 2)
+        slots[slot] = (qt, ct)
+        free = slot + 2
+    return slots
+
+
+PROJECTIONS = projection_slots()
 
 
 def last_tile_slot(g):
-    return max(ITEMS, (LAST_TILE * GROUPS + g) * GROUP + Y_LAG)
+    return max(ITEMS - 1, y_ready(LAST_TILE * GROUPS + g))
 
 
 LAST_SLOT = last_tile_slot(GROUPS - 1)
@@ -155,7 +170,7 @@ def tile_selfattention_pb_kernel(tc, q_rot, k_rot, v, v1, lamb1, lamb2, wproj, o
                 return
             g, j = divmod(h, GROUP)
             d_cols = slice(j * HEAD_DIM, (j + 1) * HEAD_DIM)
-            v1_ps = psum.tile([P, PACK, HEAD_DIM], F32, tag="x", bufs=2)
+            v1_ps = psum.tile([P, PACK, HEAD_DIM], F32, tag="o", bufs=1)
             nc.tensor.matmul(
                 out=v1_ps[:], lhsT=lamb2_diag[:], rhs=live[("v1_raw", g)][:, :, d_cols],
                 start=True, stop=True,
@@ -187,48 +202,42 @@ def tile_selfattention_pb_kernel(tc, q_rot, k_rot, v, v1, lamb1, lamb2, wproj, o
                 in_=live[("vm_grouped", h)][:].rearrange("p c t -> p (c t)"),
             )
 
-        def transpose_w(wu):
-            if not 0 <= wu < W_UNITS:
+        def transpose_w(half_unit):
+            if not 0 <= half_unit < 2 * W_UNITS:
                 return
+            wu, half = divmod(half_unit, 2)
             ct, g = divmod(wu, GROUPS)
             w_words = live[("w_raw", ct)][:].rearrange("p a k -> p (a k)").bitcast(F32)
             words_per_row = FEATURES // 2
-            for half in range(2):
-                wt_ps = psum.tile([P, 2, 2, P], F32, tag="x", bufs=2)
-                for i in range(2):
-                    for u in range(2):
-                        first = (2 * half + i) * words_per_row + (2 * g + u) * P
-                        nc.tensor.transpose(
-                            wt_ps[:, i, u, :], w_words[:, first : first + P], ident_f32[:]
-                        )
-                live[("wt_ps", wu, half)] = wt_ps
+            wt_ps = psum.tile([P, 2, 2, P], F32, tag="x", bufs=2)
+            for i in range(2):
+                for u in range(2):
+                    first = (2 * half + i) * words_per_row + (2 * g + u) * P
+                    nc.tensor.transpose(
+                        wt_ps[:, i, u, :], w_words[:, first : first + P], ident_f32[:]
+                    )
+            live[("wt_ps", half_unit)] = wt_ps
 
-        def regroup_w(wu):
-            if not 0 <= wu < W_UNITS:
+        def regroup_w(half_unit, on_vector):
+            if not 0 <= half_unit < 2 * W_UNITS or on_vector != (half_unit % 4 == 3):
                 return
-            w_grouped = work.tile([P, N_TILE, PACK], BF16, align_bytes=64, bufs=3)
+            wu, half = divmod(half_unit, 2)
+            if half == 0:
+                w_grouped = work.tile([P, N_TILE, PACK], BF16, align_bytes=64, bufs=3)
+                live[("w_grouped", wu)] = w_grouped
             grouped_words = (
-                w_grouped[:].rearrange("p c t -> p (c t)").bitcast(F32)
+                live[("w_grouped", wu)][:].rearrange("p c t -> p (c t)").bitcast(F32)
                 .rearrange("p (a c u) -> p a c u", a=ROWS_PER_COL_TILE, u=2)
             )
-            nc.scalar.copy(
-                out=grouped_words[:, 0:2, :, :],
-                in_=live[("wt_ps", wu, 0)][:].rearrange("p a u c -> p a c u"),
+            copy = nc.vector.tensor_copy if on_vector else nc.scalar.copy
+            copy(
+                out=grouped_words[:, 2 * half : 2 * half + 2, :, :],
+                in_=live[("wt_ps", half_unit)][:].rearrange("p a u c -> p a c u"),
             )
-            if wu % 2 == 0:
-                nc.scalar.copy(
-                    out=grouped_words[:, 2:4, :, :],
-                    in_=live[("wt_ps", wu, 1)][:].rearrange("p a u c -> p a c u"),
-                )
-            else:
-                nc.vector.tensor_copy(
-                    out=grouped_words[:, 2:4, :, :],
-                    in_=live[("wt_ps", wu, 1)][:].rearrange("p a u c -> p a c u"),
-                )
-            live[("w_grouped", wu)] = w_grouped
 
-        def quantise_w(wu):
-            if not 0 <= wu < W_UNITS:
+        def quantise_w(half_unit):
+            wu, half = divmod(half_unit, 2)
+            if half == 0 or not 0 <= wu < W_UNITS:
                 return
             ct, g = divmod(wu, GROUPS)
             cols = slice(ct * N_TILE, (ct + 1) * N_TILE)
@@ -242,7 +251,7 @@ def tile_selfattention_pb_kernel(tc, q_rot, k_rot, v, v1, lamb1, lamb2, wproj, o
             if not 0 <= i < ITEMS:
                 return
             qt, h = divmod(i, HEADS)
-            s_ps = psum.tile([P, TOKENS], F32, tag="s", bufs=4)
+            s_ps = psum.tile([P, TOKENS], F32, tag="s", bufs=3)
             nc.tensor.matmul(
                 out=s_ps[:],
                 lhsT=kqT[:, h, TOKEN_TILES + qt, :],
@@ -293,7 +302,7 @@ def tile_selfattention_pb_kernel(tc, q_rot, k_rot, v, v1, lamb1, lamb2, wproj, o
         def transpose_e(i):
             if not 0 <= i < ITEMS:
                 return
-            et_ps = psum.tile([P, 2, P], F32, tag="small", bufs=2)
+            et_ps = psum.tile([P, 2, P], F32, tag="e", bufs=1)
             e_words = live[("e_sb", i)][:].bitcast(F32)
             for u in range(2):
                 nc.tensor.transpose(et_ps[:, u, :], e_words[:, u * P : (u + 1) * P], ident_f32[:])
@@ -336,7 +345,7 @@ def tile_selfattention_pb_kernel(tc, q_rot, k_rot, v, v1, lamb1, lamb2, wproj, o
             if n < 0:
                 return
             g = n % GROUPS
-            y_ps = psum.tile([P, GROUP, HEAD_DIM], F32, tag="small", bufs=2)
+            y_ps = psum.tile([P, GROUP, HEAD_DIM], F32, tag="y", bufs=1)
             for j in range(GROUP):
                 h = g * GROUP + j
                 q_cols = slice(j * P, (j + 1) * P)
@@ -351,6 +360,13 @@ def tile_selfattention_pb_kernel(tc, q_rot, k_rot, v, v1, lamb1, lamb2, wproj, o
                 )
             live[("y_ps", n)] = y_ps
 
+        def invert_sums(n):
+            if n < 0:
+                return
+            inv_sum = work.tile([P, GROUP], F32)
+            nc.vector.reciprocal(out=inv_sum[:], in_=live[("row_sum", n)][:])
+            live[("inv_sum", n)] = inv_sum
+
         def normalise(n):
             if n < 0:
                 return
@@ -358,13 +374,12 @@ def tile_selfattention_pb_kernel(tc, q_rot, k_rot, v, v1, lamb1, lamb2, wproj, o
             if g == 0:
                 y_bf = work.tile([P, FEATURES], BF16)
                 live[("y_bf", qt)] = y_bf
-            inv_sum = work.tile([P, GROUP], F32)
-            nc.vector.reciprocal(out=inv_sum[:], in_=live[("row_sum", n)][:])
             for j in range(GROUP):
                 first = g * K_PASS + j * HEAD_DIM
                 nc.scalar.activation(
                     out=live[("y_bf", qt)][:, first : first + HEAD_DIM],
-                    in_=live[("y_ps", n)][:, j, :], func=ACT.Copy, scale=inv_sum[:, j : j + 1],
+                    in_=live[("y_ps", n)][:, j, :], func=ACT.Copy,
+                    scale=live[("inv_sum", n)][:, j : j + 1],
                 )
 
         def transpose_y(n):
@@ -372,7 +387,7 @@ def tile_selfattention_pb_kernel(tc, q_rot, k_rot, v, v1, lamb1, lamb2, wproj, o
                 return
             qt, g = divmod(n, GROUPS)
             y_words = live[("y_bf", qt)][:].bitcast(F32)
-            yt_ps = psum.tile([P, 2, P], F32, tag="small", bufs=2)
+            yt_ps = psum.tile([P, 2, P], F32, tag="y", bufs=1)
             for u in range(2):
                 first = (2 * g + u) * P
                 nc.tensor.transpose(yt_ps[:, u, :], y_words[:, first : first + P], ident_f32[:])
@@ -394,8 +409,8 @@ def tile_selfattention_pb_kernel(tc, q_rot, k_rot, v, v1, lamb1, lamb2, wproj, o
                 return
             qt, g = divmod(n, GROUPS)
             if g == 0:
-                y_codes = work.tile([P, GROUPS * P], U32, align_bytes=64)
-                y_scales = work.tile([P, GROUPS * P], U8, align_bytes=64)
+                y_codes = work.tile([P, GROUPS * P], U32, align_bytes=64, bufs=3)
+                y_scales = work.tile([P, GROUPS * P], U8, align_bytes=64, bufs=3)
                 live[("y_codes", qt)] = y_codes
                 live[("y_scales", qt)] = y_scales
             t_cols = slice(g * P, (g + 1) * P)
@@ -405,18 +420,17 @@ def tile_selfattention_pb_kernel(tc, q_rot, k_rot, v, v1, lamb1, lamb2, wproj, o
                 in_=live[("y_grouped", n)][:].rearrange("p q t -> p (q t)"),
             )
 
-        def project(qt, step):
-            if not 0 <= step < PROJECT_SLOTS:
+        def project(slot):
+            if slot not in PROJECTIONS:
                 return
-            ct, part = divmod(step, SLOTS_PER_COL_TILE)
+            qt, ct = PROJECTIONS[slot]
             cols = slice(ct * N_TILE, (ct + 1) * N_TILE)
-            if part == 0:
-                o_ps = psum.tile([P, N_TILE], F32, tag="x", bufs=2)
-                live[("o_ps", qt, ct)] = o_ps
-            for g in range(part * PASSES_PER_SLOT, (part + 1) * PASSES_PER_SLOT):
+            o_ps = psum.tile([P, N_TILE], F32, tag="o", bufs=1)
+            live[("o_ps", qt, ct)] = o_ps
+            for g in range(GROUPS):
                 t_cols = slice(g * P, (g + 1) * P)
                 nc.tensor.matmul_mx(
-                    out=live[("o_ps", qt, ct)][:],
+                    out=o_ps[:],
                     lhsT=live[("y_codes", qt)][:, t_cols].bitcast(FP8X4),
                     lhsT_scale=live[("y_scales", qt)][:, t_cols],
                     rhs=w_codes[:, g, cols].bitcast(FP8X4),
@@ -424,10 +438,10 @@ def tile_selfattention_pb_kernel(tc, q_rot, k_rot, v, v1, lamb1, lamb2, wproj, o
                     start=(g == 0), stop=(g == GROUPS - 1),
                 )
 
-        def store_after(qt, step):
-            done = step - STORE_LAG + 1
-            if done % SLOTS_PER_COL_TILE == 0 and 0 < done <= PROJECT_SLOTS:
-                store_out(qt, done // SLOTS_PER_COL_TILE - 1, nc.vector.tensor_copy)
+        def store_after(slot):
+            if slot in PROJECTIONS:
+                qt, ct = PROJECTIONS[slot]
+                store_out(qt, ct, nc.vector.tensor_copy)
 
         def store_out(qt, ct, copy):
             o_sb = work.tile([P, N_TILE], F32, bufs=COL_TILES)
@@ -440,7 +454,10 @@ def tile_selfattention_pb_kernel(tc, q_rot, k_rot, v, v1, lamb1, lamb2, wproj, o
             t_cols = slice(g * P, (g + 1) * P)
             for ct in range(COL_TILES):
                 if g == 0:
-                    o_ps = psum.tile([P, N_TILE], F32, tag="s", bufs=4)
+                    if ct < 2:
+                        o_ps = psum.tile([P, N_TILE], F32, tag="x", bufs=2)
+                    else:
+                        o_ps = psum.tile([P, N_TILE], F32, tag="s", bufs=3)
                     live[("o_ps", LAST_TILE, ct)] = o_ps
                 cols = slice(ct * N_TILE, (ct + 1) * N_TILE)
                 nc.tensor.matmul_mx(
@@ -462,29 +479,29 @@ def tile_selfattention_pb_kernel(tc, q_rot, k_rot, v, v1, lamb1, lamb2, wproj, o
 
         for s in range(FIRST_SLOT, LAST_SLOT + 1):
             regroup_e(s - 2)
-            regroup_w(s - W_START - 1)
-            for qt in range(LAST_TILE):
-                store_after(qt, s - project_start(qt))
+            regroup_w(s - W_START - 1, on_vector=False)
             exponentials(s)
-            keep_kq(s + 4)
-            row_maximum(s + 2)
-            quantise_e(unit_at(s - 6))
-            normalise(unit_at(s - 8))
-            regroup_y(unit_at(s - 10))
-            quantise_y(unit_at(s - 11))
-            mix_values(s - 2)
-            quantise_values(s - 3)
+            normalise(unit_at(s - 7))
+            keep_kq(s + 3)
+            row_maximum(s + 1)
+            regroup_w(s - W_START - 1, on_vector=True)
+            quantise_e(unit_at(s - 5))
+            invert_sums(unit_at(s - 6))
+            regroup_y(unit_at(s - 9))
+            quantise_y(unit_at(s - 10))
+            store_after(s - 1)
+            mix_values(s - 1)
+            quantise_values(s - 2)
             quantise_w(s - W_START - 2)
             exp_bias_of(s + 1)
-            scores(s + 3)
+            scores(s + 2)
             transpose_e(s - 1)
-            transpose_y(unit_at(s - 9))
-            transpose_kq(s + 5)
-            scale_v1(s - 1)
+            transpose_y(unit_at(s - 8))
+            transpose_kq(s + 4)
             transpose_w(s - W_START)
-            multiply_values(unit_at(s - 7))
-            for qt in range(LAST_TILE):
-                project(qt, s - project_start(qt))
+            scale_v1(s)
+            multiply_values(unit_at(s - 6))
+            project(s)
             for g in range(GROUPS):
                 if s == last_tile_slot(g):
                     project_last_tile(g)

@@ -36,9 +36,10 @@ ITEMS = TOKEN_TILES * HEADS
 UNITS = ITEMS // GROUP
 W_UNITS = COL_TILES * GROUPS
 
+WARM_UP = 4
 FIRST_SLOT = -4
-W_START = HEADS - 3
-Y_LAG = 11
+W_START = HEADS - 4
+Y_LAG = 13
 LAST_TILE = TOKEN_TILES - 1
 
 
@@ -58,20 +59,13 @@ def projection_slots():
     slots = {}
     free = 0
     for ready, qt, ct in sorted(jobs):
-        slot = max(free, ready + ready % 2)
+        slot = max(free, ready)
         slots[slot] = (qt, ct)
         free = slot + 2
     return slots
 
 
 PROJECTIONS = projection_slots()
-
-
-def last_tile_slot(g):
-    return max(ITEMS - 1, y_ready(LAST_TILE * GROUPS + g))
-
-
-LAST_SLOT = last_tile_slot(GROUPS - 1)
 
 
 def tile_selfattention_pb_kernel(tc, q_rot, k_rot, v, v1, lamb1, lamb2, wproj, out):
@@ -95,20 +89,6 @@ def tile_selfattention_pb_kernel(tc, q_rot, k_rot, v, v1, lamb1, lamb2, wproj, o
         ident_f32 = keep.tile([P, P], F32)
         make_identity(nc, ident_f32[:])
 
-        lamb1_bf = keep.tile([P, 1], BF16)
-        nc.sync.dma_start(out=lamb1_bf[:], in_=lamb1.partition_broadcast(P))
-        lamb2_bf = keep.tile([P, 1], BF16)
-        nc.sync.dma_start(out=lamb2_bf[:], in_=lamb2.partition_broadcast(P))
-        lamb1_f32 = keep.tile([P, 1], F32)
-        nc.vector.tensor_copy(out=lamb1_f32[:], in_=lamb1_bf[:])
-        lamb2_f32 = keep.tile([P, 1], F32)
-        nc.vector.tensor_copy(out=lamb2_f32[:], in_=lamb2_bf[:])
-
-        lamb2_diag = keep.tile([P, P], BF16)
-        nc.vector.tensor_scalar(
-            out=lamb2_diag[:], in0=ident_bf[:], scalar1=lamb2_f32[:, 0:1], scalar2=None, op0=ALU.mult
-        )
-
         warm = keep.tile([P, 1], F32)
         nc.scalar.activation(out=warm[:], in_=ident_f32[:, 0:1], func=ACT.Exp)
 
@@ -121,11 +101,15 @@ def tile_selfattention_pb_kernel(tc, q_rot, k_rot, v, v1, lamb1, lamb2, wproj, o
         live = {}
 
         def load_kq(g):
-            cols = slice(g * K_PASS, (g + 1) * K_PASS)
             k_raw = work.tile([P, TOKEN_TILES, K_PASS], BF16)
-            nc.sync.dma_start(out=k_raw[:], in_=k_view[:, :, cols])
             q_raw = work.tile([P, TOKEN_TILES, K_PASS], BF16)
-            nc.sync.dma_start(out=q_raw[:], in_=q_view[:, :, cols])
+            parts = 2 if g == 0 else 1
+            width = K_PASS // parts
+            for part in range(parts):
+                own = slice(part * width, (part + 1) * width)
+                cols = slice(g * K_PASS + part * width, g * K_PASS + (part + 1) * width)
+                nc.sync.dma_start(out=k_raw[:, :, own], in_=k_view[:, :, cols])
+                nc.sync.dma_start(out=q_raw[:, :, own], in_=q_view[:, :, cols])
             live[("k_raw", g)] = k_raw
             live[("q_raw", g)] = q_raw
 
@@ -302,7 +286,7 @@ def tile_selfattention_pb_kernel(tc, q_rot, k_rot, v, v1, lamb1, lamb2, wproj, o
         def transpose_e(i):
             if not 0 <= i < ITEMS:
                 return
-            et_ps = psum.tile([P, 2, P], F32, tag="e", bufs=1)
+            et_ps = psum.tile([P, 2, P], F32, tag="o" if i == ITEMS - 1 else "e", bufs=1)
             e_words = live[("e_sb", i)][:].bitcast(F32)
             for u in range(2):
                 nc.tensor.transpose(et_ps[:, u, :], e_words[:, u * P : (u + 1) * P], ident_f32[:])
@@ -345,7 +329,7 @@ def tile_selfattention_pb_kernel(tc, q_rot, k_rot, v, v1, lamb1, lamb2, wproj, o
             if n < 0:
                 return
             g = n % GROUPS
-            y_ps = psum.tile([P, GROUP, HEAD_DIM], F32, tag="y", bufs=1)
+            y_ps = psum.tile([P, GROUP, HEAD_DIM], F32, tag="x" if n == UNITS - 1 else "y", bufs=2 if n == UNITS - 1 else 1)
             for j in range(GROUP):
                 h = g * GROUP + j
                 q_cols = slice(j * P, (j + 1) * P)
@@ -420,17 +404,21 @@ def tile_selfattention_pb_kernel(tc, q_rot, k_rot, v, v1, lamb1, lamb2, wproj, o
                 in_=live[("y_grouped", n)][:].rearrange("p q t -> p (q t)"),
             )
 
-        def project(slot):
+        def project(slot, part):
             if slot not in PROJECTIONS:
                 return
             qt, ct = PROJECTIONS[slot]
             cols = slice(ct * N_TILE, (ct + 1) * N_TILE)
-            o_ps = psum.tile([P, N_TILE], F32, tag="o", bufs=1)
-            live[("o_ps", qt, ct)] = o_ps
-            for g in range(GROUPS):
+            if part == 0:
+                if slot > W_START + 2 * W_UNITS:
+                    o_ps = psum.tile([P, N_TILE], F32, tag="x", bufs=2)
+                else:
+                    o_ps = psum.tile([P, N_TILE], F32, tag="o", bufs=1)
+                live[("o_ps", qt, ct)] = o_ps
+            for g in (2 * part, 2 * part + 1):
                 t_cols = slice(g * P, (g + 1) * P)
                 nc.tensor.matmul_mx(
-                    out=o_ps[:],
+                    out=live[("o_ps", qt, ct)][:],
                     lhsT=live[("y_codes", qt)][:, t_cols].bitcast(FP8X4),
                     lhsT_scale=live[("y_scales", qt)][:, t_cols],
                     rhs=w_codes[:, g, cols].bitcast(FP8X4),
@@ -441,7 +429,7 @@ def tile_selfattention_pb_kernel(tc, q_rot, k_rot, v, v1, lamb1, lamb2, wproj, o
         def store_after(slot):
             if slot in PROJECTIONS:
                 qt, ct = PROJECTIONS[slot]
-                store_out(qt, ct, nc.vector.tensor_copy)
+                store_out(qt, ct, nc.vector.tensor_copy if slot < ITEMS - 2 else nc.scalar.copy)
 
         def store_out(qt, ct, copy):
             o_sb = work.tile([P, N_TILE], F32, bufs=COL_TILES)
@@ -454,8 +442,8 @@ def tile_selfattention_pb_kernel(tc, q_rot, k_rot, v, v1, lamb1, lamb2, wproj, o
             t_cols = slice(g * P, (g + 1) * P)
             for ct in range(COL_TILES):
                 if g == 0:
-                    if ct < 2:
-                        o_ps = psum.tile([P, N_TILE], F32, tag="x", bufs=2)
+                    if ct == 3:
+                        o_ps = psum.tile([P, N_TILE], F32, tag="o", bufs=1)
                     else:
                         o_ps = psum.tile([P, N_TILE], F32, tag="s", bufs=3)
                     live[("o_ps", LAST_TILE, ct)] = o_ps
@@ -470,6 +458,20 @@ def tile_selfattention_pb_kernel(tc, q_rot, k_rot, v, v1, lamb1, lamb2, wproj, o
                 )
 
         load_kq(0)
+        lamb1_bf = keep.tile([P, 1], BF16)
+        nc.sync.dma_start(out=lamb1_bf[:], in_=lamb1.partition_broadcast(P))
+        lamb2_bf = keep.tile([P, 1], BF16)
+        nc.sync.dma_start(out=lamb2_bf[:], in_=lamb2.partition_broadcast(P))
+        lamb1_f32 = keep.tile([P, 1], F32)
+        nc.vector.tensor_copy(out=lamb1_f32[:], in_=lamb1_bf[:])
+        lamb2_f32 = keep.tile([P, 1], F32)
+        nc.vector.tensor_copy(out=lamb2_f32[:], in_=lamb2_bf[:])
+
+        lamb2_diag = keep.tile([P, P], BF16)
+        nc.vector.tensor_scalar(
+            out=lamb2_diag[:], in0=ident_bf[:], scalar1=lamb2_f32[:, 0:1], scalar2=None, op0=ALU.mult
+        )
+
         for g in range(GROUPS):
             if g + 1 < GROUPS:
                 load_kq(g + 1)
@@ -477,33 +479,64 @@ def tile_selfattention_pb_kernel(tc, q_rot, k_rot, v, v1, lamb1, lamb2, wproj, o
         for ct in range(COL_TILES):
             load_w(ct)
 
-        for s in range(FIRST_SLOT, LAST_SLOT + 1):
+        warm_ps = psum.tile([P, TOKEN_TILES, P], F32, tag="o", bufs=1)
+        for i in range(WARM_UP):
+            nc.tensor.matmul(
+                out=warm_ps[:], lhsT=ident_bf[:],
+                rhs=ident_bf[:].unsqueeze(1).to_broadcast([P, TOKEN_TILES, P]),
+                start=True, stop=True,
+            )
+
+        for s in range(FIRST_SLOT, ITEMS):
             regroup_e(s - 2)
             regroup_w(s - W_START - 1, on_vector=False)
             exponentials(s)
-            normalise(unit_at(s - 7))
+            normalise(unit_at(s - 8))
             keep_kq(s + 3)
             row_maximum(s + 1)
-            regroup_w(s - W_START - 1, on_vector=True)
-            quantise_e(unit_at(s - 5))
+            quantise_e(unit_at(s - 6))
             invert_sums(unit_at(s - 6))
-            regroup_y(unit_at(s - 9))
-            quantise_y(unit_at(s - 10))
-            store_after(s - 1)
-            mix_values(s - 1)
-            quantise_values(s - 2)
+            regroup_y(unit_at(s - 11))
+            quantise_y(unit_at(s - 12))
+            mix_values(s - 2)
+            quantise_values(s - 3)
             quantise_w(s - W_START - 2)
+            regroup_w(s - W_START - 1, on_vector=True)
+            store_after(s - 2)
             exp_bias_of(s + 1)
             scores(s + 2)
             transpose_e(s - 1)
-            transpose_y(unit_at(s - 8))
+            if s == ITEMS - 1:
+                transpose_e(s)
+            transpose_y(unit_at(s - 10))
             transpose_kq(s + 4)
             transpose_w(s - W_START)
-            scale_v1(s)
-            multiply_values(unit_at(s - 6))
-            project(s)
-            for g in range(GROUPS):
-                if s == last_tile_slot(g):
-                    project_last_tile(g)
+            scale_v1(s - 1)
+            multiply_values(unit_at(s - 7))
+            project(s - 1, 1)
+            project(s, 0)
+
+        last = UNITS - 1
+        regroup_e(ITEMS - 2)
+        regroup_e(ITEMS - 1)
+        normalise(last - 1)
+        quantise_e(last)
+        invert_sums(last)
+        quantise_y(last - 2)
+        project(ITEMS - 1, 1)
+        transpose_y(last - 1)
+        project_last_tile(0)
+        multiply_values(last)
+        project_last_tile(1)
+        normalise(last)
+        store_after(ITEMS - 2)
+        store_after(ITEMS - 1)
+        regroup_y(last - 1)
+        quantise_y(last - 1)
+        transpose_y(last)
+        project_last_tile(2)
+        regroup_y(last)
+        quantise_y(last)
+        project_last_tile(3)
         for ct in range(COL_TILES):
             store_out(LAST_TILE, ct, nc.vector.tensor_copy if ct % 2 == 0 else nc.scalar.copy)

@@ -40,6 +40,7 @@ WARM_UP = 4
 FIRST_SLOT = -4
 W_START = HEADS - 4
 Y_LAG = 13
+ALL = range(GROUP)
 LAST_TILE = TOKEN_TILES - 1
 
 
@@ -312,53 +313,59 @@ def tile_selfattention_pb_kernel(tc, q_rot, k_rot, v, v1, lamb1, lamb2, wproj, o
                 return slot // GROUP
             return -1
 
-        def quantise_e(n):
+        def quantise_e(n, heads=ALL):
             if n < 0:
                 return
-            e_codes = work.tile([P, GROUP * P], U32, align_bytes=64)
-            e_scales = work.tile([P, GROUP * P], U8, align_bytes=64)
+            if heads[0] == 0:
+                e_codes = work.tile([P, GROUP * P], U32, align_bytes=64)
+                e_scales = work.tile([P, GROUP * P], U8, align_bytes=64)
+                live[("e_codes", n)] = e_codes
+                live[("e_scales", n)] = e_scales
+            q_cols = slice(heads[0] * P, (heads[-1] + 1) * P)
             nc.vector.quantize_mx(
-                out=e_codes[:].bitcast(FP8X4),
-                scales=e_scales[:],
-                in_=live[("e_grouped", n)][:].rearrange("p h q t -> p (h q t)"),
+                out=live[("e_codes", n)][:, q_cols].bitcast(FP8X4),
+                scales=live[("e_scales", n)][:, q_cols],
+                in_=live[("e_grouped", n)][:, heads[0] : heads[-1] + 1, :, :]
+                .rearrange("p h q t -> p (h q t)"),
             )
-            live[("e_codes", n)] = e_codes
-            live[("e_scales", n)] = e_scales
 
-        def multiply_values(n):
+        def multiply_values(n, heads=ALL):
             if n < 0:
                 return
             g = n % GROUPS
-            y_ps = psum.tile([P, GROUP, HEAD_DIM], F32, tag="x" if n == UNITS - 1 else "y", bufs=2 if n == UNITS - 1 else 1)
-            for j in range(GROUP):
+            if heads[0] == 0:
+                y_ps = psum.tile([P, GROUP, HEAD_DIM], F32, tag="x" if n == UNITS - 1 else "y", bufs=2 if n == UNITS - 1 else 1)
+                live[("y_ps", n)] = y_ps
+            for j in heads:
                 h = g * GROUP + j
                 q_cols = slice(j * P, (j + 1) * P)
                 d_cols = slice(h * HEAD_DIM, (h + 1) * HEAD_DIM)
                 nc.tensor.matmul_mx(
-                    out=y_ps[:, j, :],
+                    out=live[("y_ps", n)][:, j, :],
                     lhsT=live[("e_codes", n)][:, q_cols].bitcast(FP8X4),
                     lhsT_scale=live[("e_scales", n)][:, q_cols],
                     rhs=vm_codes[:, d_cols].bitcast(FP8X4),
                     rhs_scale=vm_scales[:, d_cols],
                     start=True, stop=True,
                 )
-            live[("y_ps", n)] = y_ps
 
-        def invert_sums(n):
+        def invert_sums(n, heads=ALL):
             if n < 0:
                 return
-            inv_sum = work.tile([P, GROUP], F32)
-            nc.vector.reciprocal(out=inv_sum[:], in_=live[("row_sum", n)][:])
-            live[("inv_sum", n)] = inv_sum
+            if heads[0] == 0:
+                inv_sum = work.tile([P, GROUP], F32)
+                live[("inv_sum", n)] = inv_sum
+            own = slice(heads[0], heads[-1] + 1)
+            nc.vector.reciprocal(out=live[("inv_sum", n)][:, own], in_=live[("row_sum", n)][:, own])
 
-        def normalise(n):
+        def normalise(n, heads=ALL):
             if n < 0:
                 return
             qt, g = divmod(n, GROUPS)
-            if g == 0:
+            if g == 0 and heads[0] == 0:
                 y_bf = work.tile([P, FEATURES], BF16)
                 live[("y_bf", qt)] = y_bf
-            for j in range(GROUP):
+            for j in heads:
                 first = g * K_PASS + j * HEAD_DIM
                 nc.scalar.activation(
                     out=live[("y_bf", qt)][:, first : first + HEAD_DIM],
@@ -489,8 +496,8 @@ def tile_selfattention_pb_kernel(tc, q_rot, k_rot, v, v1, lamb1, lamb2, wproj, o
 
         for s in range(FIRST_SLOT, ITEMS):
             regroup_e(s - 2)
-            regroup_w(s - W_START - 1, on_vector=False)
             exponentials(s)
+            regroup_w(s - W_START - 1, on_vector=False)
             normalise(unit_at(s - 8))
             keep_kq(s + 3)
             row_maximum(s + 1)
@@ -517,22 +524,27 @@ def tile_selfattention_pb_kernel(tc, q_rot, k_rot, v, v1, lamb1, lamb2, wproj, o
             project(s, 0)
 
         last = UNITS - 1
+        early, late = range(0, GROUP // 2), range(GROUP // 2, GROUP)
+        quantise_e(last, early)
+        invert_sums(last, early)
         regroup_e(ITEMS - 2)
         regroup_e(ITEMS - 1)
-        normalise(last - 1)
-        quantise_e(last)
-        invert_sums(last)
+        multiply_values(last, early)
+        quantise_e(last, late)
+        invert_sums(last, late)
         quantise_y(last - 2)
+        normalise(last - 1)
+        normalise(last, early)
         project(ITEMS - 1, 1)
         transpose_y(last - 1)
         project_last_tile(0)
-        multiply_values(last)
-        project_last_tile(1)
-        normalise(last)
+        multiply_values(last, late)
+        normalise(last, late)
         store_after(ITEMS - 2)
         store_after(ITEMS - 1)
         regroup_y(last - 1)
         quantise_y(last - 1)
+        project_last_tile(1)
         transpose_y(last)
         project_last_tile(2)
         regroup_y(last)

@@ -204,7 +204,7 @@ def tile_selfattention_pb_kernel(tc, q_rot, k_rot, v, v1, lamb1, lamb2, wproj, o
             live[("wt_ps", half_unit)] = wt_ps
 
         def regroup_w(half_unit, on_vector):
-            if not 0 <= half_unit < 2 * W_UNITS or on_vector != (half_unit % 4 == 3):
+            if not 0 <= half_unit < 2 * W_UNITS or on_vector != (half_unit % 4 == 9):
                 return
             wu, half = divmod(half_unit, 2)
             if half == 0:
@@ -359,7 +359,7 @@ def tile_selfattention_pb_kernel(tc, q_rot, k_rot, v, v1, lamb1, lamb2, wproj, o
             nc.vector.reciprocal(out=live[("inv_sum", n)][:, own], in_=live[("row_sum", n)][:, own])
 
         def normalise(n, heads=ALL):
-            if n < 0:
+            if n < 0 or (n < 14):
                 return
             qt, g = divmod(n, GROUPS)
             if g == 0 and heads[0] == 0:
@@ -372,6 +372,21 @@ def tile_selfattention_pb_kernel(tc, q_rot, k_rot, v, v1, lamb1, lamb2, wproj, o
                     in_=live[("y_ps", n)][:, j, :], func=ACT.Copy,
                     scale=live[("inv_sum", n)][:, j : j + 1],
                 )
+
+        def normalise_v(n):
+            if n < 0 or not (n < 14):
+                return
+            qt, g = divmod(n, GROUPS)
+            if g == 0:
+                y_bf = work.tile([P, FEATURES], BF16)
+                live[("y_bf", qt)] = y_bf
+            nc.vector.tensor_tensor(
+                out=live[("y_bf", qt)][:, g * K_PASS : (g + 1) * K_PASS]
+                .rearrange("q (h d) -> q h d", h=GROUP),
+                in0=live[("y_ps", n)][:],
+                in1=live[("inv_sum", n)][:].unsqueeze(2).to_broadcast([P, GROUP, HEAD_DIM]),
+                op=ALU.mult,
+            )
 
         def transpose_y(n):
             if n < 0:
@@ -509,6 +524,7 @@ def tile_selfattention_pb_kernel(tc, q_rot, k_rot, v, v1, lamb1, lamb2, wproj, o
             quantise_values(s - 3)
             quantise_w(s - W_START - 2)
             regroup_w(s - W_START - 1, on_vector=True)
+            normalise_v(unit_at(s - 8))
             store_after(s - 2)
             exp_bias_of(s + 1)
             scores(s + 2)

@@ -93,7 +93,12 @@ def tile_selfattention_pb_kernel(tc, q_rot, k_rot, v, v1, lamb1, lamb2, wproj, o
         warm = keep.tile([P, 1], F32)
         nc.scalar.activation(out=warm[:], in_=ident_f32[:, 0:1], func=ACT.Exp)
 
-        kqT = keep.tile([P, HEADS, 2 * TOKEN_TILES, P], BF16)
+        kqT = keep.tile([P, HEADS, TOKEN_TILES + 1, P], BF16)
+        qT = keep.tile([P, TOKEN_TILES - 1, HEADS, P], BF16)
+        k_raw = keep.tile([P, TOKEN_TILES, FEATURES], BF16)
+        q_raw = keep.tile([P, TOKEN_TILES, FEATURES], BF16)
+        v_raw = keep.tile([P, PACK, FEATURES], BF16)
+        v1_raw = keep.tile([P, PACK, FEATURES], BF16)
         vm_codes = keep.tile([P, FEATURES], U32, align_bytes=64)
         vm_scales = keep.tile([P, FEATURES], U8, align_bytes=64)
         w_codes = keep.tile([P, GROUPS, OUT_FEATURES], U32, align_bytes=64)
@@ -101,48 +106,38 @@ def tile_selfattention_pb_kernel(tc, q_rot, k_rot, v, v1, lamb1, lamb2, wproj, o
 
         live = {}
 
-        def load_kq(g):
-            k_raw = work.tile([P, TOKEN_TILES, K_PASS], BF16)
-            q_raw = work.tile([P, TOKEN_TILES, K_PASS], BF16)
-            parts = 2 if g == 0 else 1
-            width = K_PASS // parts
-            for part in range(parts):
-                own = slice(part * width, (part + 1) * width)
-                cols = slice(g * K_PASS + part * width, g * K_PASS + (part + 1) * width)
-                nc.sync.dma_start(out=k_raw[:, :, own], in_=k_view[:, :, cols])
-                nc.sync.dma_start(out=q_raw[:, :, own], in_=q_view[:, :, cols])
-            live[("k_raw", g)] = k_raw
-            live[("q_raw", g)] = q_raw
+        def columns(first_head, heads):
+            return slice(first_head * HEAD_DIM, (first_head + heads) * HEAD_DIM)
 
-        def load_values(g):
-            cols = slice(g * K_PASS, (g + 1) * K_PASS)
-            v1_raw = work.tile([P, PACK, K_PASS], BF16, bufs=3)
-            for u in range(2):
-                nc.sync.dma_start(out=v1_raw[:, 2 * u : 2 * u + 2, :], in_=v1_view[:, u, :, cols])
-            v_raw = work.tile([P, PACK, K_PASS], BF16, bufs=3)
-            for u in range(2):
-                nc.sync.dma_start(out=v_raw[:, 2 * u : 2 * u + 2, :], in_=v_view[:, u, :, cols])
-            live[("v1_raw", g)] = v1_raw
-            live[("v_raw", g)] = v_raw
+        def load_k(first_head, heads):
+            cols = columns(first_head, heads)
+            nc.sync.dma_start(out=k_raw[:, :, cols], in_=k_view[:, :, cols])
 
-        def load_w(ct):
-            w_raw = work.tile([P, ROWS_PER_COL_TILE, FEATURES], BF16)
+        def load_q(qt, first_head, heads):
+            cols = columns(first_head, heads)
+            nc.sync.dma_start(out=q_raw[:, qt, cols], in_=q_view[:, qt, cols])
+
+        def load_values(first_head, heads):
+            cols = columns(first_head, heads)
+            for raw, view in ((v1_raw, v1_view), (v_raw, v_view)):
+                for u in range(2):
+                    nc.sync.dma_start(out=raw[:, 2 * u : 2 * u + 2, cols], in_=view[:, u, :, cols])
+
+        def load_w(ct, half):
+            w_raw = work.tile([P, ROWS_PER_COL_TILE, FEATURES // 2], BF16, bufs=3)
             rows = slice(ct * ROWS_PER_COL_TILE, (ct + 1) * ROWS_PER_COL_TILE)
-            nc.sync.dma_start(out=w_raw[:], in_=w_view[:, rows, :])
-            live[("w_raw", ct)] = w_raw
+            cols = slice(half * FEATURES // 2, (half + 1) * FEATURES // 2)
+            nc.sync.dma_start(out=w_raw[:], in_=w_view[:, rows, cols])
+            live[("w_raw", ct, half)] = w_raw
 
         def transpose_kq(h):
             if not 0 <= h < HEADS:
                 return
-            g, j = divmod(h, GROUP)
-            d_cols = slice(j * HEAD_DIM, (j + 1) * HEAD_DIM)
-            kq_ps = psum.tile([P, 2 * TOKEN_TILES, P], BF16, tag="x", bufs=2)
+            cols = columns(h, 1)
+            kq_ps = psum.tile([P, TOKEN_TILES + 1, P], BF16, tag="x", bufs=2)
             for a in range(TOKEN_TILES):
-                nc.tensor.transpose(kq_ps[:, a, :], live[("k_raw", g)][:, a, d_cols], ident_bf[:])
-            for a in range(TOKEN_TILES):
-                nc.tensor.transpose(
-                    kq_ps[:, TOKEN_TILES + a, :], live[("q_raw", g)][:, a, d_cols], ident_bf[:]
-                )
+                nc.tensor.transpose(kq_ps[:, a, :], k_raw[:, a, cols], ident_bf[:])
+            nc.tensor.transpose(kq_ps[:, TOKEN_TILES, :], q_raw[:, 0, cols], ident_bf[:])
             live[("kq_ps", h)] = kq_ps
 
         def keep_kq(h):
@@ -150,14 +145,39 @@ def tile_selfattention_pb_kernel(tc, q_rot, k_rot, v, v1, lamb1, lamb2, wproj, o
                 return
             nc.scalar.copy(out=kqT[:, h, :, :], in_=live[("kq_ps", h)][:])
 
+        def transpose_q(n):
+            if not GROUPS <= n < UNITS:
+                return
+            qt, g = divmod(n, GROUPS)
+            q_ps = psum.tile([P, GROUP, P], BF16, tag="y", bufs=1)
+            for j in range(GROUP):
+                nc.tensor.transpose(
+                    q_ps[:, j, :], q_raw[:, qt, columns(g * GROUP + j, 1)], ident_bf[:]
+                )
+            live[("q_ps", n)] = q_ps
+
+        def keep_q(n):
+            if not GROUPS <= n < UNITS:
+                return
+            qt, g = divmod(n, GROUPS)
+            nc.scalar.copy(
+                out=qT[:, qt - 1, g * GROUP : (g + 1) * GROUP, :], in_=live[("q_ps", n)][:]
+            )
+
+        def prepare_mix():
+            nc.vector.tensor_copy(out=lamb1_f32[:], in_=lamb1_bf[:])
+            nc.vector.tensor_copy(out=lamb2_f32[:], in_=lamb2_bf[:])
+            nc.vector.tensor_scalar(
+                out=lamb2_diag[:], in0=ident_bf[:], scalar1=lamb2_f32[:, 0:1], scalar2=None,
+                op0=ALU.mult,
+            )
+
         def scale_v1(h):
             if not 0 <= h < HEADS:
                 return
-            g, j = divmod(h, GROUP)
-            d_cols = slice(j * HEAD_DIM, (j + 1) * HEAD_DIM)
             v1_ps = psum.tile([P, PACK, HEAD_DIM], F32, tag="o", bufs=1)
             nc.tensor.matmul(
-                out=v1_ps[:], lhsT=lamb2_diag[:], rhs=live[("v1_raw", g)][:, :, d_cols],
+                out=v1_ps[:], lhsT=lamb2_diag[:], rhs=v1_raw[:, :, columns(h, 1)],
                 start=True, stop=True,
             )
             live[("scaled_v1", h)] = v1_ps
@@ -165,12 +185,10 @@ def tile_selfattention_pb_kernel(tc, q_rot, k_rot, v, v1, lamb1, lamb2, wproj, o
         def mix_values(h):
             if not 0 <= h < HEADS:
                 return
-            g, j = divmod(h, GROUP)
-            d_cols = slice(j * HEAD_DIM, (j + 1) * HEAD_DIM)
             vm_grouped = work.tile([P, HEAD_DIM, PACK], BF16, align_bytes=64)
             nc.vector.scalar_tensor_tensor(
                 out=vm_grouped[:],
-                in0=live[("v_raw", g)][:, :, d_cols].rearrange("p t c -> p c t"),
+                in0=v_raw[:, :, columns(h, 1)].rearrange("p t c -> p c t"),
                 scalar=lamb1_f32[:, 0:1],
                 in1=live[("scaled_v1", h)][:].rearrange("p t c -> p c t"),
                 op0=ALU.mult, op1=ALU.add,
@@ -192,12 +210,12 @@ def tile_selfattention_pb_kernel(tc, q_rot, k_rot, v, v1, lamb1, lamb2, wproj, o
                 return
             wu, half = divmod(half_unit, 2)
             ct, g = divmod(wu, GROUPS)
-            w_words = live[("w_raw", ct)][:].rearrange("p a k -> p (a k)").bitcast(F32)
-            words_per_row = FEATURES // 2
+            w_words = live[("w_raw", ct, g // 2)][:].rearrange("p a k -> p (a k)").bitcast(F32)
+            words_per_row = FEATURES // 4
             wt_ps = psum.tile([P, 2, 2, P], F32, tag="x", bufs=2)
             for i in range(2):
                 for u in range(2):
-                    first = (2 * half + i) * words_per_row + (2 * g + u) * P
+                    first = (2 * half + i) * words_per_row + (2 * (g % 2) + u) * P
                     nc.tensor.transpose(
                         wt_ps[:, i, u, :], w_words[:, first : first + P], ident_f32[:]
                     )
@@ -239,7 +257,7 @@ def tile_selfattention_pb_kernel(tc, q_rot, k_rot, v, v1, lamb1, lamb2, wproj, o
             s_ps = psum.tile([P, TOKENS], F32, tag="s", bufs=3)
             nc.tensor.matmul(
                 out=s_ps[:],
-                lhsT=kqT[:, h, TOKEN_TILES + qt, :],
+                lhsT=kqT[:, h, TOKEN_TILES, :] if qt == 0 else qT[:, qt - 1, h, :],
                 rhs=kqT[:, h, 0:TOKEN_TILES, :].rearrange("p a t -> p (a t)"),
                 start=True, stop=True,
             )
@@ -313,6 +331,9 @@ def tile_selfattention_pb_kernel(tc, q_rot, k_rot, v, v1, lamb1, lamb2, wproj, o
                 return slot // GROUP
             return -1
 
+        def unit_of(item):
+            return item // GROUP if item % GROUP == 0 else -1
+
         def quantise_e(n, heads=ALL):
             if n < 0:
                 return
@@ -359,7 +380,7 @@ def tile_selfattention_pb_kernel(tc, q_rot, k_rot, v, v1, lamb1, lamb2, wproj, o
             nc.vector.reciprocal(out=live[("inv_sum", n)][:, own], in_=live[("row_sum", n)][:, own])
 
         def normalise(n, heads=ALL):
-            if n < 0 or (n < 14):
+            if n < 0 or (3 <= n < 14):
                 return
             qt, g = divmod(n, GROUPS)
             if g == 0 and heads[0] == 0:
@@ -374,7 +395,7 @@ def tile_selfattention_pb_kernel(tc, q_rot, k_rot, v, v1, lamb1, lamb2, wproj, o
                 )
 
         def normalise_v(n):
-            if n < 0 or not (n < 14):
+            if n < 0 or not (3 <= n < 14):
                 return
             qt, g = divmod(n, GROUPS)
             if g == 0:
@@ -479,27 +500,30 @@ def tile_selfattention_pb_kernel(tc, q_rot, k_rot, v, v1, lamb1, lamb2, wproj, o
                     start=(g == 0), stop=(g == GROUPS - 1),
                 )
 
-        load_kq(0)
+        load_k(0, 2)
+        load_q(0, 0, 4)
+        load_k(2, 2)
         lamb1_bf = keep.tile([P, 1], BF16)
         nc.sync.dma_start(out=lamb1_bf[:], in_=lamb1.partition_broadcast(P))
         lamb2_bf = keep.tile([P, 1], BF16)
         nc.sync.dma_start(out=lamb2_bf[:], in_=lamb2.partition_broadcast(P))
         lamb1_f32 = keep.tile([P, 1], F32)
-        nc.vector.tensor_copy(out=lamb1_f32[:], in_=lamb1_bf[:])
         lamb2_f32 = keep.tile([P, 1], F32)
-        nc.vector.tensor_copy(out=lamb2_f32[:], in_=lamb2_bf[:])
-
         lamb2_diag = keep.tile([P, P], BF16)
-        nc.vector.tensor_scalar(
-            out=lamb2_diag[:], in0=ident_bf[:], scalar1=lamb2_f32[:, 0:1], scalar2=None, op0=ALU.mult
-        )
-
-        for g in range(GROUPS):
-            if g + 1 < GROUPS:
-                load_kq(g + 1)
-            load_values(g)
-        for ct in range(COL_TILES):
-            load_w(ct)
+        load_k(4, 4)
+        load_q(0, 4, 12)
+        load_values(0, 4)
+        load_k(8, 8)
+        load_values(4, 4)
+        load_values(8, 8)
+        load_w(0, 0)
+        load_q(1, 0, HEADS)
+        load_w(0, 1)
+        for ct in range(1, COL_TILES):
+            load_w(ct, 0)
+            if ct < COL_TILES - 1:
+                load_q(ct + 1, 0, HEADS)
+            load_w(ct, 1)
 
         warm_ps = psum.tile([P, TOKEN_TILES, P], F32, tag="o", bufs=1)
         for i in range(WARM_UP):
@@ -511,20 +535,23 @@ def tile_selfattention_pb_kernel(tc, q_rot, k_rot, v, v1, lamb1, lamb2, wproj, o
 
         for s in range(FIRST_SLOT, ITEMS):
             regroup_e(s - 2)
+            keep_q(unit_of(s + 6))
             exponentials(s)
             regroup_w(s - W_START - 1, on_vector=False)
             normalise(unit_at(s - 8))
             keep_kq(s + 3)
             row_maximum(s + 1)
+            if s == 0:
+                prepare_mix()
+            quantise_values(s - 3)
             quantise_e(unit_at(s - 6))
             invert_sums(unit_at(s - 6))
             regroup_y(unit_at(s - 11))
             quantise_y(unit_at(s - 12))
             mix_values(s - 2)
-            quantise_values(s - 3)
+            normalise_v(unit_at(s - 8))
             quantise_w(s - W_START - 2)
             regroup_w(s - W_START - 1, on_vector=True)
-            normalise_v(unit_at(s - 8))
             store_after(s - 2)
             exp_bias_of(s + 1)
             scores(s + 2)
@@ -532,12 +559,13 @@ def tile_selfattention_pb_kernel(tc, q_rot, k_rot, v, v1, lamb1, lamb2, wproj, o
             if s == ITEMS - 1:
                 transpose_e(s)
             transpose_y(unit_at(s - 10))
+            transpose_q(unit_of(s + 7))
             transpose_kq(s + 4)
             transpose_w(s - W_START)
-            scale_v1(s - 1)
             multiply_values(unit_at(s - 7))
             project(s - 1, 1)
             project(s, 0)
+            scale_v1(s - 1)
 
         last = UNITS - 1
         early, late = range(0, GROUP // 2), range(GROUP // 2, GROUP)

@@ -36,6 +36,7 @@ ITEMS = TOKEN_TILES * HEADS
 UNITS = ITEMS // GROUP
 W_UNITS = COL_TILES * GROUPS
 
+FILL_N = 256
 WARM_UP = 4
 FIRST_SLOT = -4
 W_START = HEADS - 4
@@ -469,6 +470,17 @@ def tile_selfattention_pb_kernel(tc, q_rot, k_rot, v, v1, lamb1, lamb2, wproj, o
                     start=(g == 0), stop=(g == GROUPS - 1),
                 )
 
+        def fill(slot):
+            if not (HEADS < slot < ITEMS - 8) or any(slot - i in PROJECTIONS for i in range(3)):
+                return
+            fill_ps = psum.tile([P, FILL_N], F32, tag="o", bufs=1)
+            nc.tensor.matmul_mx(
+                out=fill_ps[:],
+                lhsT=vm_codes[:, 0:P].bitcast(FP8X4), lhsT_scale=vm_scales[:, 0:P],
+                rhs=vm_codes[:, 0:FILL_N].bitcast(FP8X4), rhs_scale=vm_scales[:, 0:FILL_N],
+                start=True, stop=True,
+            )
+
         def store_after(slot):
             if slot in PROJECTIONS:
                 qt, ct = PROJECTIONS[slot]
@@ -516,8 +528,8 @@ def tile_selfattention_pb_kernel(tc, q_rot, k_rot, v, v1, lamb1, lamb2, wproj, o
         load_k(8, 8)
         load_values(4, 4)
         load_values(8, 8)
-        load_w(0, 0)
         load_q(1, 0, HEADS)
+        load_w(0, 0)
         load_w(0, 1)
         for ct in range(1, COL_TILES):
             load_w(ct, 0)
@@ -565,6 +577,7 @@ def tile_selfattention_pb_kernel(tc, q_rot, k_rot, v, v1, lamb1, lamb2, wproj, o
             multiply_values(unit_at(s - 7))
             project(s - 1, 1)
             project(s, 0)
+            fill(s)
             scale_v1(s - 1)
 
         last = UNITS - 1

@@ -40,13 +40,23 @@ FILL_N = 256
 WARM_UP = 4
 FIRST_SLOT = -4
 W_START = HEADS - 4
+FIRST_QUICK = 11
 Y_LAG = 13
 ALL = range(GROUP)
 LAST_TILE = TOKEN_TILES - 1
 
 
+def stage_slot(n, lag):
+    hurry = 0 if n < FIRST_QUICK else 1 if lag < 9 else 2
+    if n == FIRST_QUICK and lag < 9:
+        hurry = 0
+    elif n == FIRST_QUICK:
+        hurry = 1
+    return n * GROUP + lag - hurry
+
+
 def y_ready(n):
-    return n * GROUP + Y_LAG
+    return stage_slot(n, Y_LAG)
 
 
 def w_ready(ct):
@@ -150,7 +160,7 @@ def tile_selfattention_pb_kernel(tc, q_rot, k_rot, v, v1, lamb1, lamb2, wproj, o
             if not GROUPS <= n < UNITS:
                 return
             qt, g = divmod(n, GROUPS)
-            q_ps = psum.tile([P, GROUP, P], BF16, tag="y", bufs=1)
+            q_ps = psum.tile([P, GROUP, P], BF16, tag="o" if n >= 14 else "y", bufs=1)
             for j in range(GROUP):
                 nc.tensor.transpose(
                     q_ps[:, j, :], q_raw[:, qt, columns(g * GROUP + j, 1)], ident_bf[:]
@@ -163,14 +173,6 @@ def tile_selfattention_pb_kernel(tc, q_rot, k_rot, v, v1, lamb1, lamb2, wproj, o
             qt, g = divmod(n, GROUPS)
             nc.scalar.copy(
                 out=qT[:, qt - 1, g * GROUP : (g + 1) * GROUP, :], in_=live[("q_ps", n)][:]
-            )
-
-        def prepare_mix():
-            nc.vector.tensor_copy(out=lamb1_f32[:], in_=lamb1_bf[:])
-            nc.vector.tensor_copy(out=lamb2_f32[:], in_=lamb2_bf[:])
-            nc.vector.tensor_scalar(
-                out=lamb2_diag[:], in0=ident_bf[:], scalar1=lamb2_f32[:, 0:1], scalar2=None,
-                op0=ALU.mult,
             )
 
         def scale_v1(h):
@@ -327,9 +329,10 @@ def tile_selfattention_pb_kernel(tc, q_rot, k_rot, v, v1, lamb1, lamb2, wproj, o
                 out=grouped_words[:, j, :, :], in_=live[("et_ps", i)][:].rearrange("p u q -> p q u")
             )
 
-        def unit_at(slot):
-            if slot % GROUP == 0 and 0 <= slot < ITEMS:
-                return slot // GROUP
+        def unit_at(slot, lag):
+            for n in range(UNITS):
+                if slot == stage_slot(n, lag):
+                    return n
             return -1
 
         def unit_of(item):
@@ -381,7 +384,7 @@ def tile_selfattention_pb_kernel(tc, q_rot, k_rot, v, v1, lamb1, lamb2, wproj, o
             nc.vector.reciprocal(out=live[("inv_sum", n)][:, own], in_=live[("row_sum", n)][:, own])
 
         def normalise(n, heads=ALL):
-            if n < 0 or (3 <= n < 14):
+            if n < 0 or (3 <= n < 15):
                 return
             qt, g = divmod(n, GROUPS)
             if g == 0 and heads[0] == 0:
@@ -396,7 +399,7 @@ def tile_selfattention_pb_kernel(tc, q_rot, k_rot, v, v1, lamb1, lamb2, wproj, o
                 )
 
         def normalise_v(n):
-            if n < 0 or not (3 <= n < 14):
+            if n < 0 or not (3 <= n < 15):
                 return
             qt, g = divmod(n, GROUPS)
             if g == 0:
@@ -471,7 +474,9 @@ def tile_selfattention_pb_kernel(tc, q_rot, k_rot, v, v1, lamb1, lamb2, wproj, o
                 )
 
         def fill(slot):
-            if not (HEADS < slot < ITEMS - 8) or any(slot - i in PROJECTIONS for i in range(3)):
+            if not (HEADS < slot < ITEMS - 8) or any(slot - i in PROJECTIONS for i in range(3)) or (
+                slot > W_START + 2 * W_UNITS and slot % GROUP == 1
+            ):
                 return
             fill_ps = psum.tile([P, FILL_N], F32, tag="o", bufs=1)
             nc.tensor.matmul_mx(
@@ -484,7 +489,7 @@ def tile_selfattention_pb_kernel(tc, q_rot, k_rot, v, v1, lamb1, lamb2, wproj, o
         def store_after(slot):
             if slot in PROJECTIONS:
                 qt, ct = PROJECTIONS[slot]
-                store_out(qt, ct, nc.vector.tensor_copy if slot < ITEMS - 2 else nc.scalar.copy)
+                store_out(qt, ct, nc.scalar.copy if slot >= 50 else nc.vector.tensor_copy)
 
         def store_out(qt, ct, copy):
             o_sb = work.tile([P, N_TILE], F32, bufs=COL_TILES)
@@ -520,8 +525,15 @@ def tile_selfattention_pb_kernel(tc, q_rot, k_rot, v, v1, lamb1, lamb2, wproj, o
         lamb2_bf = keep.tile([P, 1], BF16)
         nc.sync.dma_start(out=lamb2_bf[:], in_=lamb2.partition_broadcast(P))
         lamb1_f32 = keep.tile([P, 1], F32)
+        nc.vector.tensor_copy(out=lamb1_f32[:], in_=lamb1_bf[:])
         lamb2_f32 = keep.tile([P, 1], F32)
+        nc.vector.tensor_copy(out=lamb2_f32[:], in_=lamb2_bf[:])
+
         lamb2_diag = keep.tile([P, P], BF16)
+        nc.vector.tensor_scalar(
+            out=lamb2_diag[:], in0=ident_bf[:], scalar1=lamb2_f32[:, 0:1], scalar2=None, op0=ALU.mult
+        )
+
         load_k(4, 4)
         load_q(0, 4, 12)
         load_values(0, 4)
@@ -550,18 +562,16 @@ def tile_selfattention_pb_kernel(tc, q_rot, k_rot, v, v1, lamb1, lamb2, wproj, o
             keep_q(unit_of(s + 6))
             exponentials(s)
             regroup_w(s - W_START - 1, on_vector=False)
-            normalise(unit_at(s - 8))
+            normalise(unit_at(s, 8))
             keep_kq(s + 3)
             row_maximum(s + 1)
-            if s == 0:
-                prepare_mix()
             quantise_values(s - 3)
-            quantise_e(unit_at(s - 6))
-            invert_sums(unit_at(s - 6))
-            regroup_y(unit_at(s - 11))
-            quantise_y(unit_at(s - 12))
+            quantise_e(unit_at(s, 6))
+            invert_sums(unit_at(s, 6))
+            regroup_y(unit_at(s, 11))
+            quantise_y(unit_at(s, 12))
             mix_values(s - 2)
-            normalise_v(unit_at(s - 8))
+            normalise_v(unit_at(s, 8))
             quantise_w(s - W_START - 2)
             regroup_w(s - W_START - 1, on_vector=True)
             store_after(s - 2)
@@ -570,11 +580,11 @@ def tile_selfattention_pb_kernel(tc, q_rot, k_rot, v, v1, lamb1, lamb2, wproj, o
             transpose_e(s - 1)
             if s == ITEMS - 1:
                 transpose_e(s)
-            transpose_y(unit_at(s - 10))
+            transpose_y(unit_at(s, 10))
             transpose_q(unit_of(s + 7))
             transpose_kq(s + 4)
             transpose_w(s - W_START)
-            multiply_values(unit_at(s - 7))
+            multiply_values(unit_at(s, 7))
             project(s - 1, 1)
             project(s, 0)
             fill(s)
@@ -584,23 +594,21 @@ def tile_selfattention_pb_kernel(tc, q_rot, k_rot, v, v1, lamb1, lamb2, wproj, o
         early, late = range(0, GROUP // 2), range(GROUP // 2, GROUP)
         quantise_e(last, early)
         invert_sums(last, early)
+        transpose_y(last - 1)
         regroup_e(ITEMS - 2)
         regroup_e(ITEMS - 1)
         multiply_values(last, early)
+        regroup_y(last - 1)
         quantise_e(last, late)
         invert_sums(last, late)
-        quantise_y(last - 2)
-        normalise(last - 1)
-        normalise(last, early)
+        quantise_y(last - 1)
         project(ITEMS - 1, 1)
-        transpose_y(last - 1)
+        store_after(ITEMS - 2)
+        normalise(last, early)
         project_last_tile(0)
         multiply_values(last, late)
         normalise(last, late)
-        store_after(ITEMS - 2)
         store_after(ITEMS - 1)
-        regroup_y(last - 1)
-        quantise_y(last - 1)
         project_last_tile(1)
         transpose_y(last)
         project_last_tile(2)

@@ -36,7 +36,6 @@ ITEMS = TOKEN_TILES * HEADS
 UNITS = ITEMS // GROUP
 W_UNITS = COL_TILES * GROUPS
 
-FILL_N = 256
 WARM_UP = 4
 FIRST_SLOT = -4
 W_START = HEADS - 4
@@ -473,19 +472,6 @@ def tile_selfattention_pb_kernel(tc, q_rot, k_rot, v, v1, lamb1, lamb2, wproj, o
                     start=(g == 0), stop=(g == GROUPS - 1),
                 )
 
-        def fill(slot):
-            if not (HEADS < slot < ITEMS - 8) or any(slot - i in PROJECTIONS for i in range(3)) or (
-                slot > W_START + 2 * W_UNITS and slot % GROUP == 1
-            ):
-                return
-            fill_ps = psum.tile([P, FILL_N], F32, tag="o", bufs=1)
-            nc.tensor.matmul_mx(
-                out=fill_ps[:],
-                lhsT=vm_codes[:, 0:P].bitcast(FP8X4), lhsT_scale=vm_scales[:, 0:P],
-                rhs=vm_codes[:, 0:FILL_N].bitcast(FP8X4), rhs_scale=vm_scales[:, 0:FILL_N],
-                start=True, stop=True,
-            )
-
         def store_after(slot):
             if slot in PROJECTIONS:
                 qt, ct = PROJECTIONS[slot]
@@ -587,7 +573,6 @@ def tile_selfattention_pb_kernel(tc, q_rot, k_rot, v, v1, lamb1, lamb2, wproj, o
             multiply_values(unit_at(s, 7))
             project(s - 1, 1)
             project(s, 0)
-            fill(s)
             scale_v1(s - 1)
 
         last = UNITS - 1

@@ -521,13 +521,17 @@ def tile_selfattention_pb_kernel(tc, q_rot, k_rot, v, v1, lamb1, lamb2, wproj, o
         )
 
         load_k(4, 4)
-        load_q(0, 4, 12)
+        load_q(0, 4, 4)
         load_values(0, 4)
-        load_k(8, 8)
+        load_q(0, 8, 8)
+        load_k(8, 4)
         load_values(4, 4)
-        load_values(8, 8)
-        load_q(1, 0, HEADS)
+        load_q(1, 0, 4)
+        load_k(12, 4)
+        load_values(8, 4)
         load_w(0, 0)
+        load_q(1, 4, 12)
+        load_values(12, 4)
         load_w(0, 1)
         for ct in range(1, COL_TILES):
             load_w(ct, 0)

import math
from contextlib import ExitStack

import concourse.mybir as mybir
from concourse.masks import make_identity

BF16 = mybir.dt.bfloat16
F32 = mybir.dt.float32
U32 = mybir.dt.uint32
U8 = mybir.dt.uint8
FP8X4 = mybir.dt.float8_e4m3fn_x4
ACT = mybir.ActivationFunctionType
ALU = mybir.AluOpType
AXIS = mybir.AxisListType

P = 128
PACK = 4
K_PASS = P * PACK
TOKENS = 512
TOKEN_TILES = TOKENS // P
HEADS = 16
HEAD_DIM = 128
FEATURES = HEADS * HEAD_DIM
GROUP = K_PASS // HEAD_DIM
GROUPS = HEADS // GROUP
OUT_FEATURES = 2048
N_TILE = 512
COL_TILES = OUT_FEATURES // N_TILE
ROWS_PER_COL_TILE = N_TILE // P
SCALE = 1.0 / math.sqrt(HEAD_DIM)

FLOPS = 2 * 2 * HEADS * TOKENS * TOKENS * HEAD_DIM + 2 * TOKENS * FEATURES * OUT_FEATURES


ITEMS = TOKEN_TILES * HEADS
UNITS = ITEMS // GROUP
W_UNITS = COL_TILES * GROUPS

WARM_UP = 4
FIRST_SLOT = -4
W_START = HEADS - 4
FIRST_QUICK = 11
Y_LAG = 13
ALL = range(GROUP)
LAST_TILE = TOKEN_TILES - 1


def stage_slot(n, lag):
    hurry = 0 if n < FIRST_QUICK else 1 if lag < 9 else 2
    if n == FIRST_QUICK and lag < 9:
        hurry = 0
    elif n == FIRST_QUICK:
        hurry = 1
    return n * GROUP + lag - hurry


def y_ready(n):
    return stage_slot(n, Y_LAG)


def w_ready(ct):
    return W_START + 2 * (ct + 1) * GROUPS + 2


def projection_slots():
    jobs = []
    for qt in range(LAST_TILE):
        for ct in range(COL_TILES):
            jobs.append((max(y_ready(qt * GROUPS + GROUPS - 1), w_ready(ct)), qt, ct))
    slots = {}
    free = 0
    for ready, qt, ct in sorted(jobs):
        slot = max(free, ready)
        slots[slot] = (qt, ct)
        free = slot + 2
    return slots


PROJECTIONS = projection_slots()


def tile_selfattention_pb_kernel(tc, q_rot, k_rot, v, v1, lamb1, lamb2, wproj, out):
    nc = tc.nc

    q_view = q_rot.rearrange("b (a p) h d -> p (b a) (h d)", p=P)
    k_view = k_rot.rearrange("b (a p) h d -> p (b a) (h d)", p=P)
    v_view = v.rearrange("b (u p e) h d -> p (b u) e (h d)", u=2, e=2)
    v1_view = v1.rearrange("b (u p e) h d -> p (b u) e (h d)", u=2, e=2)
    w_view = wproj.rearrange("(a p) k -> p a k", p=P)
    out_view = out.rearrange("b (a p) c -> p (b a) c", p=P)

    with ExitStack() as ctx:
        keep = ctx.enter_context(tc.tile_pool(name="keep", bufs=1))
        work = ctx.enter_context(tc.tile_pool(name="work", bufs=2))
        psum = ctx.enter_context(tc.psum_pool(name="psum", bufs=1))
        ctx.enter_context(tc.manual_schedule())

        ident_bf = keep.tile([P, P], BF16)
        make_identity(nc, ident_bf[:])
        ident_f32 = keep.tile([P, P], F32)
        make_identity(nc, ident_f32[:])

        warm = keep.tile([P, 1], F32)
        nc.scalar.activation(out=warm[:], in_=ident_f32[:, 0:1], func=ACT.Exp)

        kqT = keep.tile([P, HEADS, TOKEN_TILES + 1, P], BF16)
        qT = keep.tile([P, TOKEN_TILES - 1, HEADS, P], BF16)
        k_raw = keep.tile([P, TOKEN_TILES, FEATURES], BF16)
        q_raw = keep.tile([P, TOKEN_TILES, FEATURES], BF16)
        v_raw = keep.tile([P, PACK, FEATURES], BF16)
        v1_raw = keep.tile([P, PACK, FEATURES], BF16)
        vm_codes = keep.tile([P, FEATURES], U32, align_bytes=64)
        vm_scales = keep.tile([P, FEATURES], U8, align_bytes=64)
        w_codes = keep.tile([P, GROUPS, OUT_FEATURES], U32, align_bytes=64)
        w_scales = keep.tile([P, GROUPS, OUT_FEATURES], U8, align_bytes=64)

        live = {}

        def columns(first_head, heads):
            return slice(first_head * HEAD_DIM, (first_head + heads) * HEAD_DIM)

        def load_k(first_head, heads):
            cols = columns(first_head, heads)
            nc.sync.dma_start(out=k_raw[:, :, cols], in_=k_view[:, :, cols])

        def load_q(qt, first_head, heads):
            cols = columns(first_head, heads)
            nc.sync.dma_start(out=q_raw[:, qt, cols], in_=q_view[:, qt, cols])

        def load_values(first_head, heads):
            cols = columns(first_head, heads)
            for raw, view in ((v1_raw, v1_view), (v_raw, v_view)):
                for u in range(2):
                    nc.sync.dma_start(out=raw[:, 2 * u : 2 * u + 2, cols], in_=view[:, u, :, cols])

        def load_w(ct, half):
            w_raw = work.tile([P, ROWS_PER_COL_TILE, FEATURES // 2], BF16, bufs=3)
            rows = slice(ct * ROWS_PER_COL_TILE, (ct + 1) * ROWS_PER_COL_TILE)
            cols = slice(half * FEATURES // 2, (half + 1) * FEATURES // 2)
            nc.sync.dma_start(out=w_raw[:], in_=w_view[:, rows, cols])
            live[("w_raw", ct, half)] = w_raw

        def transpose_kq(h):
            if not 0 <= h < HEADS:
                return
            cols = columns(h, 1)
            kq_ps = psum.tile([P, TOKEN_TILES + 1, P], BF16, tag="x", bufs=2)
            for a in range(TOKEN_TILES):
                nc.tensor.transpose(kq_ps[:, a, :], k_raw[:, a, cols], ident_bf[:])
            nc.tensor.transpose(kq_ps[:, TOKEN_TILES, :], q_raw[:, 0, cols], ident_bf[:])
            live[("kq_ps", h)] = kq_ps

        def keep_kq(h):
            if not 0 <= h < HEADS:
                return
            nc.scalar.copy(out=kqT[:, h, :, :], in_=live[("kq_ps", h)][:])

        def transpose_q(n):
            if not GROUPS <= n < UNITS:
                return
            qt, g = divmod(n, GROUPS)
            q_ps = psum.tile([P, GROUP, P], BF16, tag="o" if n >= 14 else "y", bufs=1)
            for j in range(GROUP):
                nc.tensor.transpose(
                    q_ps[:, j, :], q_raw[:, qt, columns(g * GROUP + j, 1)], ident_bf[:]
                )
            live[("q_ps", n)] = q_ps

        def keep_q(n):
            if not GROUPS <= n < UNITS:
                return
            qt, g = divmod(n, GROUPS)
            nc.scalar.copy(
                out=qT[:, qt - 1, g * GROUP : (g + 1) * GROUP, :], in_=live[("q_ps", n)][:]
            )

        def scale_v1(h):
            if not 0 <= h < HEADS:
                return
            v1_ps = psum.tile([P, PACK, HEAD_DIM], F32, tag="o", bufs=1)
            nc.tensor.matmul(
                out=v1_ps[:], lhsT=lamb2_diag[:], rhs=v1_raw[:, :, columns(h, 1)],
                start=True, stop=True,
            )
            live[("scaled_v1", h)] = v1_ps

        def mix_values(h):
            if not 0 <= h < HEADS:
                return
            vm_grouped = work.tile([P, HEAD_DIM, PACK], BF16, align_bytes=64)
            nc.vector.scalar_tensor_tensor(
                out=vm_grouped[:],
                in0=v_raw[:, :, columns(h, 1)].rearrange("p t c -> p c t"),
                scalar=lamb1_f32[:, 0:1],
                in1=live[("scaled_v1", h)][:].rearrange("p t c -> p c t"),
                op0=ALU.mult, op1=ALU.add,
            )
            live[("vm_grouped", h)] = vm_grouped

        def quantise_values(h):
            if not 0 <= h < HEADS:
                return
            cols = slice(h * HEAD_DIM, (h + 1) * HEAD_DIM)
            nc.vector.quantize_mx(
                out=vm_codes[:, cols].bitcast(FP8X4),
                scales=vm_scales[:, cols],
                in_=live[("vm_grouped", h)][:].rearrange("p c t -> p (c t)"),
            )

        def transpose_w(half_unit):
            if not 0 <= half_unit < 2 * W_UNITS:
                return
            wu, half = divmod(half_unit, 2)
            ct, g = divmod(wu, GROUPS)
            w_words = live[("w_raw", ct, g // 2)][:].rearrange("p a k -> p (a k)").bitcast(F32)
            words_per_row = FEATURES // 4
            wt_ps = psum.tile([P, 2, 2, P], F32, tag="x", bufs=2)
            for i in range(2):
                for u in range(2):
                    first = (2 * half + i) * words_per_row + (2 * (g % 2) + u) * P
                    nc.tensor.transpose(
                        wt_ps[:, i, u, :], w_words[:, first : first + P], ident_f32[:]
                    )
            live[("wt_ps", half_unit)] = wt_ps

        def regroup_w(half_unit, on_vector):
            if not 0 <= half_unit < 2 * W_UNITS or on_vector != (half_unit % 4 == 9):
                return
            wu, half = divmod(half_unit, 2)
            if half == 0:
                w_grouped = work.tile([P, N_TILE, PACK], BF16, align_bytes=64, bufs=3)
                live[("w_grouped", wu)] = w_grouped
            grouped_words = (
                live[("w_grouped", wu)][:].rearrange("p c t -> p (c t)").bitcast(F32)
                .rearrange("p (a c u) -> p a c u", a=ROWS_PER_COL_TILE, u=2)
            )
            copy = nc.vector.tensor_copy if on_vector else nc.scalar.copy
            copy(
                out=grouped_words[:, 2 * half : 2 * half + 2, :, :],
                in_=live[("wt_ps", half_unit)][:].rearrange("p a u c -> p a c u"),
            )

        def quantise_w(half_unit):
            wu, half = divmod(half_unit, 2)
            if half == 0 or not 0 <= wu < W_UNITS:
                return
            ct, g = divmod(wu, GROUPS)
            cols = slice(ct * N_TILE, (ct + 1) * N_TILE)
            nc.vector.quantize_mx(
                out=w_codes[:, g, cols].bitcast(FP8X4),
                scales=w_scales[:, g, cols],
                in_=live[("w_grouped", wu)][:].rearrange("p c t -> p (c t)"),
            )

        def scores(i):
            if not 0 <= i < ITEMS:
                return
            qt, h = divmod(i, HEADS)
            s_ps = psum.tile([P, TOKENS], F32, tag="s", bufs=3)
            nc.tensor.matmul(
                out=s_ps[:],
                lhsT=kqT[:, h, TOKEN_TILES, :] if qt == 0 else qT[:, qt - 1, h, :],
                rhs=kqT[:, h, 0:TOKEN_TILES, :].rearrange("p a t -> p (a t)"),
                start=True, stop=True,
            )
            live[("s_ps", i)] = s_ps

        def row_maximum(i):
            if not 0 <= i < ITEMS:
                return
            n, j = divmod(i, GROUP)
            if j == 0:
                row_max = work.tile([P, GROUP], F32)
                live[("row_max", n)] = row_max
            nc.vector.reduce_max(
                out=live[("row_max", n)][:, j : j + 1], in_=live[("s_ps", i)][:], axis=AXIS.X
            )

        def exp_bias_of(i):
            if not 0 <= i < ITEMS:
                return
            n, j = divmod(i, GROUP)
            if j == 0:
                exp_bias = work.tile([P, GROUP], F32)
                live[("exp_bias", n)] = exp_bias
            nc.gpsimd.tensor_scalar(
                out=live[("exp_bias", n)][:, j : j + 1],
                in0=live[("row_max", n)][:, j : j + 1],
                scalar1=-SCALE, scalar2=0.0, op0=ALU.mult, op1=ALU.add,
            )

        def exponentials(i):
            if not 0 <= i < ITEMS:
                return
            n, j = divmod(i, GROUP)
            if j == 0:
                row_sum = work.tile([P, GROUP], F32, bufs=3)
                live[("row_sum", n)] = row_sum
            e_sb = work.tile([P, TOKENS], BF16, bufs=3)
            nc.scalar.activation(
                out=e_sb[:], in_=live[("s_ps", i)][:], func=ACT.Exp,
                bias=live[("exp_bias", n)][:, j : j + 1], scale=SCALE,
                accum_out=live[("row_sum", n)][:, j : j + 1],
            )
            live[("e_sb", i)] = e_sb

        def transpose_e(i):
            if not 0 <= i < ITEMS:
                return
            et_ps = psum.tile([P, 2, P], F32, tag="o" if i == ITEMS - 1 else "e", bufs=1)
            e_words = live[("e_sb", i)][:].bitcast(F32)
            for u in range(2):
                nc.tensor.transpose(et_ps[:, u, :], e_words[:, u * P : (u + 1) * P], ident_f32[:])
            live[("et_ps", i)] = et_ps

        def regroup_e(i):
            if not 0 <= i < ITEMS:
                return
            n, j = divmod(i, GROUP)
            if j == 0:
                e_grouped = work.tile([P, GROUP, P, PACK], BF16, align_bytes=64)
                live[("e_grouped", n)] = e_grouped
            grouped_words = (
                live[("e_grouped", n)][:].rearrange("p h q t -> p (h q t)").bitcast(F32)
                .rearrange("p (h q u) -> p h q u", h=GROUP, u=2)
            )
            nc.scalar.copy(
                out=grouped_words[:, j, :, :], in_=live[("et_ps", i)][:].rearrange("p u q -> p q u")
            )

        def unit_at(slot, lag):
            for n in range(UNITS):
                if slot == stage_slot(n, lag):
                    return n
            return -1

        def unit_of(item):
            return item // GROUP if item % GROUP == 0 else -1

        def quantise_e(n, heads=ALL):
            if n < 0:
                return
            if heads[0] == 0:
                e_codes = work.tile([P, GROUP * P], U32, align_bytes=64)
                e_scales = work.tile([P, GROUP * P], U8, align_bytes=64)
                live[("e_codes", n)] = e_codes
                live[("e_scales", n)] = e_scales
            q_cols = slice(heads[0] * P, (heads[-1] + 1) * P)
            nc.vector.quantize_mx(
                out=live[("e_codes", n)][:, q_cols].bitcast(FP8X4),
                scales=live[("e_scales", n)][:, q_cols],
                in_=live[("e_grouped", n)][:, heads[0] : heads[-1] + 1, :, :]
                .rearrange("p h q t -> p (h q t)"),
            )

        def multiply_values(n, heads=ALL):
            if n < 0:
                return
            g = n % GROUPS
            if heads[0] == 0:
                y_ps = psum.tile([P, GROUP, HEAD_DIM], F32, tag="x" if n == UNITS - 1 else "y", bufs=2 if n == UNITS - 1 else 1)
                live[("y_ps", n)] = y_ps
            for j in heads:
                h = g * GROUP + j
                q_cols = slice(j * P, (j + 1) * P)
                d_cols = slice(h * HEAD_DIM, (h + 1) * HEAD_DIM)
                nc.tensor.matmul_mx(
                    out=live[("y_ps", n)][:, j, :],
                    lhsT=live[("e_codes", n)][:, q_cols].bitcast(FP8X4),
                    lhsT_scale=live[("e_scales", n)][:, q_cols],
                    rhs=vm_codes[:, d_cols].bitcast(FP8X4),
                    rhs_scale=vm_scales[:, d_cols],
                    start=True, stop=True,
                )

        def invert_sums(n, heads=ALL):
            if n < 0:
                return
            if heads[0] == 0:
                inv_sum = work.tile([P, GROUP], F32)
                live[("inv_sum", n)] = inv_sum
            own = slice(heads[0], heads[-1] + 1)
            nc.vector.reciprocal(out=live[("inv_sum", n)][:, own], in_=live[("row_sum", n)][:, own])

        def normalise(n, heads=ALL):
            if n < 0 or (3 <= n < 15):
                return
            qt, g = divmod(n, GROUPS)
            if g == 0 and heads[0] == 0:
                y_bf = work.tile([P, FEATURES], BF16)
                live[("y_bf", qt)] = y_bf
            for j in heads:
                first = g * K_PASS + j * HEAD_DIM
                nc.scalar.activation(
                    out=live[("y_bf", qt)][:, first : first + HEAD_DIM],
                    in_=live[("y_ps", n)][:, j, :], func=ACT.Copy,
                    scale=live[("inv_sum", n)][:, j : j + 1],
                )

        def normalise_v(n):
            if n < 0 or not (3 <= n < 15):
                return
            qt, g = divmod(n, GROUPS)
            if g == 0:
                y_bf = work.tile([P, FEATURES], BF16)
                live[("y_bf", qt)] = y_bf
            nc.vector.tensor_tensor(
                out=live[("y_bf", qt)][:, g * K_PASS : (g + 1) * K_PASS]
                .rearrange("q (h d) -> q h d", h=GROUP),
                in0=live[("y_ps", n)][:],
                in1=live[("inv_sum", n)][:].unsqueeze(2).to_broadcast([P, GROUP, HEAD_DIM]),
                op=ALU.mult,
            )

        def transpose_y(n):
            if n < 0:
                return
            qt, g = divmod(n, GROUPS)
            y_words = live[("y_bf", qt)][:].bitcast(F32)
            yt_ps = psum.tile([P, 2, P], F32, tag="y", bufs=1)
            for u in range(2):
                first = (2 * g + u) * P
                nc.tensor.transpose(yt_ps[:, u, :], y_words[:, first : first + P], ident_f32[:])
            live[("yt_ps", n)] = yt_ps

        def regroup_y(n):
            if n < 0:
                return
            y_grouped = work.tile([P, P, PACK], BF16, align_bytes=64)
            nc.vector.tensor_copy(
                out=y_grouped[:].rearrange("p q t -> p (q t)").bitcast(F32)
                .rearrange("p (q u) -> p q u", u=2),
                in_=live[("yt_ps", n)][:].rearrange("p u q -> p q u"),
            )
            live[("y_grouped", n)] = y_grouped

        def quantise_y(n):
            if n < 0:
                return
            qt, g = divmod(n, GROUPS)
            if g == 0:
                y_codes = work.tile([P, GROUPS * P], U32, align_bytes=64, bufs=3)
                y_scales = work.tile([P, GROUPS * P], U8, align_bytes=64, bufs=3)
                live[("y_codes", qt)] = y_codes
                live[("y_scales", qt)] = y_scales
            t_cols = slice(g * P, (g + 1) * P)
            nc.vector.quantize_mx(
                out=live[("y_codes", qt)][:, t_cols].bitcast(FP8X4),
                scales=live[("y_scales", qt)][:, t_cols],
                in_=live[("y_grouped", n)][:].rearrange("p q t -> p (q t)"),
            )

        def project(slot, part):
            if slot not in PROJECTIONS:
                return
            qt, ct = PROJECTIONS[slot]
            cols = slice(ct * N_TILE, (ct + 1) * N_TILE)
            if part == 0:
                if slot > W_START + 2 * W_UNITS:
                    o_ps = psum.tile([P, N_TILE], F32, tag="x", bufs=2)
                else:
                    o_ps = psum.tile([P, N_TILE], F32, tag="o", bufs=1)
                live[("o_ps", qt, ct)] = o_ps
            for g in (2 * part, 2 * part + 1):
                t_cols = slice(g * P, (g + 1) * P)
                nc.tensor.matmul_mx(
                    out=live[("o_ps", qt, ct)][:],
                    lhsT=live[("y_codes", qt)][:, t_cols].bitcast(FP8X4),
                    lhsT_scale=live[("y_scales", qt)][:, t_cols],
                    rhs=w_codes[:, g, cols].bitcast(FP8X4),
                    rhs_scale=w_scales[:, g, cols],
                    start=(g == 0), stop=(g == GROUPS - 1),
                )

        def store_after(slot):
            if slot in PROJECTIONS:
                qt, ct = PROJECTIONS[slot]
                store_out(qt, ct, nc.scalar.copy if slot >= 50 else nc.vector.tensor_copy)

        def store_out(qt, ct, copy):
            o_sb = work.tile([P, N_TILE], F32, bufs=COL_TILES)
            copy(out=o_sb[:], in_=live[("o_ps", qt, ct)][:])
            nc.sync.dma_start(out=out_view[:, qt, ct * N_TILE : (ct + 1) * N_TILE], in_=o_sb[:])

        def project_last_tile(g):
            if not 0 <= g < GROUPS:
                return
            t_cols = slice(g * P, (g + 1) * P)
            for ct in range(COL_TILES):
                if g == 0:
                    if ct == 3:
                        o_ps = psum.tile([P, N_TILE], F32, tag="o", bufs=1)
                    else:
                        o_ps = psum.tile([P, N_TILE], F32, tag="s", bufs=3)
                    live[("o_ps", LAST_TILE, ct)] = o_ps
                cols = slice(ct * N_TILE, (ct + 1) * N_TILE)
                nc.tensor.matmul_mx(
                    out=live[("o_ps", LAST_TILE, ct)][:],
                    lhsT=live[("y_codes", LAST_TILE)][:, t_cols].bitcast(FP8X4),
                    lhsT_scale=live[("y_scales", LAST_TILE)][:, t_cols],
                    rhs=w_codes[:, g, cols].bitcast(FP8X4),
                    rhs_scale=w_scales[:, g, cols],
                    start=(g == 0), stop=(g == GROUPS - 1),
                )

        load_k(0, 2)
        load_q(0, 0, 4)
        load_k(2, 2)
        lamb1_bf = keep.tile([P, 1], BF16)
        nc.sync.dma_start(out=lamb1_bf[:], in_=lamb1.partition_broadcast(P))
        lamb2_bf = keep.tile([P, 1], BF16)
        nc.sync.dma_start(out=lamb2_bf[:], in_=lamb2.partition_broadcast(P))
        lamb1_f32 = keep.tile([P, 1], F32)
        nc.vector.tensor_copy(out=lamb1_f32[:], in_=lamb1_bf[:])
        lamb2_f32 = keep.tile([P, 1], F32)
        nc.vector.tensor_copy(out=lamb2_f32[:], in_=lamb2_bf[:])

        lamb2_diag = keep.tile([P, P], BF16)
        nc.vector.tensor_scalar(
            out=lamb2_diag[:], in0=ident_bf[:], scalar1=lamb2_f32[:, 0:1], scalar2=None, op0=ALU.mult
        )

        load_k(4, 4)
        load_q(0, 4, 4)
        load_values(0, 4)
        load_q(0, 8, 8)
        load_k(8, 4)
        load_values(4, 4)
        load_q(1, 0, 4)
        load_k(12, 4)
        load_values(8, 4)
        load_w(0, 0)
        load_q(1, 4, 12)
        load_values(12, 4)
        load_w(0, 1)
        for ct in range(1, COL_TILES):
            load_w(ct, 0)
            if ct < COL_TILES - 1:
                load_q(ct + 1, 0, HEADS)
            load_w(ct, 1)

        warm_ps = psum.tile([P, TOKEN_TILES, P], F32, tag="o", bufs=1)
        for i in range(WARM_UP):
            nc.tensor.matmul(
                out=warm_ps[:], lhsT=ident_bf[:],
                rhs=ident_bf[:].unsqueeze(1).to_broadcast([P, TOKEN_TILES, P]),
                start=True, stop=True,
            )

        for s in range(FIRST_SLOT, ITEMS):
            regroup_e(s - 2)
            keep_q(unit_of(s + 6))
            exponentials(s)
            regroup_w(s - W_START - 1, on_vector=False)
            normalise(unit_at(s, 8))
            keep_kq(s + 3)
            row_maximum(s + 1)
            quantise_values(s - 3)
            quantise_e(unit_at(s, 6))
            invert_sums(unit_at(s, 6))
            regroup_y(unit_at(s, 11))
            quantise_y(unit_at(s, 12))
            mix_values(s - 2)
            normalise_v(unit_at(s, 8))
            quantise_w(s - W_START - 2)
            regroup_w(s - W_START - 1, on_vector=True)
            store_after(s - 2)
            exp_bias_of(s + 1)
            scores(s + 2)
            transpose_e(s - 1)
            if s == ITEMS - 1:
                transpose_e(s)
            transpose_y(unit_at(s, 10))
            transpose_q(unit_of(s + 7))
            transpose_kq(s + 4)
            transpose_w(s - W_START)
            multiply_values(unit_at(s, 7))
            project(s - 1, 1)
            project(s, 0)
            scale_v1(s - 1)

        last = UNITS - 1
        early, late = range(0, GROUP // 2), range(GROUP // 2, GROUP)
        quantise_e(last, early)
        invert_sums(last, early)
        transpose_y(last - 1)
        regroup_e(ITEMS - 2)
        regroup_e(ITEMS - 1)
        multiply_values(last, early)
        regroup_y(last - 1)
        quantise_e(last, late)
        invert_sums(last, late)
        quantise_y(last - 1)
        project(ITEMS - 1, 1)
        store_after(ITEMS - 2)
        normalise(last, early)
        project_last_tile(0)
        multiply_values(last, late)
        normalise(last, late)
        store_after(ITEMS - 1)
        project_last_tile(1)
        transpose_y(last)
        project_last_tile(2)
        regroup_y(last)
        quantise_y(last)
        project_last_tile(3)
        for ct in range(COL_TILES):
            store_out(LAST_TILE, ct, nc.vector.tensor_copy if ct % 2 == 0 else nc.scalar.copy)
